import numpy as np
import ml_dtypes


def mxq(x, axis, fmt="e4m3"):
    dtype, down = {"e4m3": (ml_dtypes.float8_e4m3fn, 7), "e5m2": (ml_dtypes.float8_e5m2, 14)}[fmt]
    v = np.moveaxis(np.asarray(x, np.float32).astype(ml_dtypes.bfloat16).astype(np.float64), axis, -1)
    blocks = v.reshape(v.shape[:-1] + (-1, 32))
    amax = np.abs(blocks).max(-1, keepdims=True)
    byte = np.maximum(np.where(amax > 0, np.frexp(amax)[1] - 1 + 127, 0) - down, 1)
    scale = np.exp2(byte - 127.0)
    codes = (blocks / scale).astype(np.float32).astype(dtype).astype(np.float64)
    return np.moveaxis((codes * scale).reshape(v.shape), -1, axis)


WIDE = False


def mx_kscale(k):
    if not WIDE:
        return np.ones(k)
    levels = np.array([10, -10, 5, -5, 0])
    a = np.random.permutation(np.resize(levels, k // 512 * 4)).reshape(k // 512, 4)
    idx = np.arange(k)
    return np.exp2(a[idx // 512, idx % 128 // 32])


BF16 = ml_dtypes.bfloat16


def bf(x):
    return np.asarray(x, np.float32).astype(BF16)


def f64(x):
    return np.asarray(x).astype(np.float64)


E2M1 = np.array([0.0, 0.5, 1.0, 1.5, 2.0, 3.0, 4.0, 6.0, -0.0, -0.5, -1.0, -1.5, -2.0, -3.0, -4.0, -6.0])


def pack_weight(w, fmt):
    k, n = w.shape
    w = f64(bf(w)).reshape(k // 32, 32, n)
    amax = np.abs(w).max(1)
    if fmt == "e4m3":
        byte = np.frexp(amax)[1] - 1 + 127 - 7
    else:
        mant, ex = np.frexp(amax / 6.0)
        byte = np.where(mant > 0.5, ex, ex - 1) + 127
    byte = np.clip(np.where(amax > 0, byte, 1), 1, 254)
    scaled = (w * np.exp2(127.0 - byte)[:, None, :]).reshape(k, n).astype(np.float32)
    by_word = np.ascontiguousarray(scaled.reshape(k // 512, 128, 4, n).transpose(0, 1, 3, 2))
    if fmt == "e4m3":
        words = by_word.astype(ml_dtypes.float8_e4m3fn).view(np.uint8)
    else:
        c = by_word.astype(ml_dtypes.float4_e2m1fn).view(np.uint8) & 0xF
        words = c[..., 0::2] | (c[..., 1::2] << 4)
    return np.ascontiguousarray(words), np.ascontiguousarray(byte.astype(np.uint8).reshape(k // 512, 16, n))


def unpack_weight(words, scales, fmt):
    g, p, n, _ = words.shape
    if fmt == "e4m3":
        vals = np.ascontiguousarray(words).view(ml_dtypes.float8_e4m3fn).astype(np.float64)
    else:
        nib = np.empty((g, p, n, 4), np.uint8)
        nib[..., 0::2] = words & 0xF
        nib[..., 1::2] = words >> 4
        vals = E2M1[nib]
    vals = vals * np.repeat(np.exp2(scales.astype(np.float64) - 127.0), 8, axis=1)[..., None]
    return vals.transpose(0, 1, 3, 2).reshape(g * 512, n)


B, S, H, D = 16, 256, 2, 512
GAMMA = 64.0
L = 1


def squash(v):
    return v / (1.0 + np.abs(v))


def setup_inputs():
    s = mx_kscale(D)
    hq1 = bf(np.random.standard_normal((B, H, S, D)) * 0.25 * s)
    hk1 = bf(np.random.standard_normal((B, H, S, D)) * 0.25 * s)
    stack = np.random.standard_normal((1, H, D, D)) * 0.75 / np.sqrt(D) / s[:, None]
    words, scales = pack_weight(stack.reshape(-1, D), "e4m3")
    bias1 = bf(np.random.standard_normal((1, H, 1, D)) * 0.1)
    return {"hq1": hq1,
            "hk1": hk1,
            "proj1_words": words,
            "proj1_scales": scales,
            "bias1": bias1}


def reference(hq1, hk1, proj1_words, proj1_scales, bias1):
    pq = unpack_weight(proj1_words, proj1_scales, "e4m3").reshape(L, H, D, D)
    hq = ((mxq(f64(hq1), 3, "e4m3") @ pq) + f64(bias1)) + f64(hq1)
    hk = ((mxq(f64(hk1), 3, "e4m3") @ pq) + f64(bias1)) + f64(hk1)
    qh = squash(hq * GAMMA)
    kh = squash(hk * GAMMA)
    return mxq(qh, 3, "e4m3") @ mxq(kh, 3, "e4m3").transpose(0, 1, 3, 2)

@@ -1,0 +1,168 @@
+from contextlib import ExitStack
+
+import concourse.masks as masks
+import concourse.mybir as mybir
+
+F32 = mybir.dt.float32
+BF16 = mybir.dt.bfloat16
+I32 = mybir.dt.int32
+U8 = mybir.dt.uint8
+U32 = mybir.dt.uint32
+FP8X4 = mybir.dt.float8_e4m3fn_x4
+ACT = mybir.ActivationFunctionType
+ALU = mybir.AluOpType
+
+P = 128
+PACK = 4
+B, H, S, D = 16, 2, 256, 512
+ROWS = 2 * S
+ROW_TILES = ROWS // P
+CHUNKS = D // P
+GAMMA = 64.0
+
+FLOPS = 2 * (2 * B * H * S * D * D) + 2 * B * H * S * S * D
+
+
+def tile_decoder_pb_t_e_kernel(tc, hq1, hk1, proj1_words, proj1_scales, bias1, out):
+    nc = tc.nc
+    with ExitStack() as ctx:
+        const = ctx.enter_context(tc.tile_pool(name="const", bufs=1))
+
+        ident_f32 = const.tile([P, P], F32, name="ident_f32")
+        masks.make_identity(nc, ident_f32[:])
+        ident_bf16 = const.tile([P, P], BF16, name="ident_bf16")
+        masks.make_identity(nc, ident_bf16[:])
+        inv_gamma = const.tile([P, 1], F32, name="inv_gamma")
+        nc.vector.memset(inv_gamma[:], 1.0 / GAMMA)
+
+        w_words = const.tile([P, H, D * PACK], U8, name="w_words", align_bytes=64)
+        for h in range(H):
+            nc.sync.dma_start(
+                out=w_words[:, h, :].bitcast(I32),
+                in_=proj1_words[h].rearrange("p n t -> p (n t)").bitcast(I32),
+            )
+        w_scales = const.tile([P, H, D], U8, name="w_scales", align_bytes=64)
+        nc.vector.memset(w_scales[:].rearrange("p h n -> p (h n)").bitcast(I32), 0)
+        for quadrant in range(4):
+            nc.sync.dma_start(
+                out=w_scales[32 * quadrant : 32 * quadrant + 4, :, :].bitcast(I32),
+                in_=proj1_scales[:, 4 * quadrant : 4 * quadrant + 4, :].rearrange("h r n -> r h n").bitcast(I32),
+            )
+
+        bias_rows = const.tile([P, P], BF16, name="bias_rows")
+        nc.vector.memset(bias_rows[:], 0.0)
+        nc.sync.dma_start(
+            out=bias_rows[0 : H * CHUNKS, :],
+            in_=bias1.rearrange("a h c (m j) -> (a h c m) j", j=P),
+        )
+        bias_col = const.tile([P, H * CHUNKS], F32, name="bias_col")
+        with tc.psum_pool(name="setup_psum", bufs=1) as setup_psum:
+            bias_ps = setup_psum.tile([P, P], BF16, name="bias_ps")
+            nc.tensor.transpose(bias_ps[:], bias_rows[:], ident_bf16[:])
+            nc.vector.tensor_copy(out=bias_col[:], in_=bias_ps[:, 0 : H * CHUNKS])
+
+        loads = ctx.enter_context(tc.tile_pool(name="loads", bufs=3))
+        work = ctx.enter_context(tc.tile_pool(name="work", bufs=2))
+        stores = ctx.enter_context(tc.tile_pool(name="stores", bufs=2))
+        words_psum = ctx.enter_context(tc.psum_pool(name="words_psum", bufs=2))
+        plain_psum = ctx.enter_context(tc.psum_pool(name="plain_psum", bufs=2))
+        proj_psum = ctx.enter_context(tc.psum_pool(name="proj_psum", bufs=3))
+        score_psum = ctx.enter_context(tc.psum_pool(name="score_psum", bufs=1))
+
+        for b in range(B):
+            xq_b = loads.tile([P, H * S // P, D], BF16, name="xq_b")
+            nc.sync.dma_start(out=xq_b[:], in_=hq1[b].rearrange("h (i p) d -> p (h i) d", p=P))
+            xk_b = loads.tile([P, H * S // P, D], BF16, name="xk_b")
+            nc.sync.dma_start(out=xk_b[:], in_=hk1[b].rearrange("h (i p) d -> p (h i) d", p=P))
+            scores_b = stores.tile([P, H * S // P, S], F32, name="scores_b")
+
+            for h in range(H):
+                row_tiles = [xq_b[:, 2 * h, :], xq_b[:, 2 * h + 1, :], xk_b[:, 2 * h, :], xk_b[:, 2 * h + 1, :]]
+
+                x_grouped = work.tile([P, ROWS * PACK], BF16, name="x_grouped", align_bytes=64)
+                x_grouped_words = x_grouped[:].bitcast(F32).rearrange("p (s u) -> p s u", u=2)
+                for half in range(2):
+                    words_ps = words_psum.tile([P, 2, S], F32, name="words_ps")
+                    for i in range(2):
+                        words = row_tiles[2 * half + i].bitcast(F32)
+                        for u in range(2):
+                            nc.tensor.transpose(
+                                words_ps[:, u, P * i : P * (i + 1)], words[:, u : D // 2 : 2], ident_f32[:]
+                            )
+                    nc.vector.tensor_copy(
+                        out=x_grouped_words[:, S * half : S * (half + 1), :],
+                        in_=words_ps[:].rearrange("p u s -> p s u"),
+                    )
+
+                x_plain = work.tile([P, CHUNKS, ROWS], BF16, name="x_plain")
+                for pair in range(2):
+                    plain_ps = plain_psum.tile([P, 2, ROWS], BF16, name="plain_ps")
+                    for mm in range(2):
+                        m = 2 * pair + mm
+                        for r in range(ROW_TILES):
+                            nc.tensor.transpose(
+                                plain_ps[:, mm, P * r : P * (r + 1)],
+                                row_tiles[r][:, P * m : P * (m + 1)],
+                                ident_bf16[:],
+                            )
+                    nc.scalar.copy(out=x_plain[:, 2 * pair : 2 * pair + 2, :], in_=plain_ps[:])
+
+                x_codes = work.tile([P, ROWS], U32, name="x_codes", align_bytes=64)
+                x_scales = work.tile([P, ROWS], U8, name="x_scales", align_bytes=64)
+                nc.vector.quantize_mx(out=x_codes[:].bitcast(FP8X4), scales=x_scales[:], in_=x_grouped[:])
+
+                z = work.tile([P, CHUNKS, ROWS], F32, name="z")
+                for m in range(CHUNKS):
+                    proj_ps = proj_psum.tile([P, ROWS], F32, name="proj_ps")
+                    nc.tensor.matmul_mx(
+                        out=proj_ps[:],
+                        lhsT=w_words[:, h, P * PACK * m : P * PACK * (m + 1)].bitcast(FP8X4),
+                        lhsT_scale=w_scales[:, h, P * m : P * (m + 1)],
+                        rhs=x_codes[:].bitcast(FP8X4),
+                        rhs_scale=x_scales[:],
+                        start=True,
+                        stop=True,
+                    )
+                    nc.vector.scalar_tensor_tensor(
+                        out=z[:, m, :],
+                        in0=proj_ps[:],
+                        scalar=bias_col[:, CHUNKS * h + m : CHUNKS * h + m + 1],
+                        in1=x_plain[:, m, :],
+                        op0=ALU.add,
+                        op1=ALU.add,
+                    )
+
+                z_by_column = z[:].rearrange("p m s -> p s m")
+                magnitude = work.tile([P, ROWS, CHUNKS], F32, name="magnitude")
+                nc.scalar.activation(out=magnitude[:], in_=z_by_column, func=ACT.Abs)
+                rsqrt = work.tile([P, ROWS, CHUNKS], F32, name="rsqrt")
+                nc.scalar.activation(
+                    out=rsqrt[:], in_=magnitude[:], func=ACT.Abs_reciprocal_sqrt, bias=inv_gamma[:, 0:1], scale=1.0
+                )
+                recip = work.tile([P, ROWS, CHUNKS], F32, name="recip")
+                nc.scalar.activation(out=recip[:], in_=rsqrt[:], func=ACT.Square)
+                squashed = work.tile([P, ROWS, CHUNKS], BF16, name="squashed", align_bytes=64)
+                nc.vector.tensor_tensor(out=squashed[:], in0=z_by_column, in1=recip[:], op=ALU.mult)
+
+                s_codes = work.tile([P, ROWS], U32, name="s_codes", align_bytes=64)
+                s_scales = work.tile([P, ROWS], U8, name="s_scales", align_bytes=64)
+                nc.vector.quantize_mx(
+                    out=s_codes[:].bitcast(FP8X4),
+                    scales=s_scales[:],
+                    in_=squashed[:].rearrange("p s m -> p (s m)"),
+                )
+
+                score_ps = score_psum.tile([P, S // P, S], F32, name="score_ps")
+                for i in range(S // P):
+                    nc.tensor.matmul_mx(
+                        out=score_ps[:, i, :],
+                        lhsT=s_codes[:, P * i : P * (i + 1)].bitcast(FP8X4),
+                        lhsT_scale=s_scales[:, P * i : P * (i + 1)],
+                        rhs=s_codes[:, S : 2 * S].bitcast(FP8X4),
+                        rhs_scale=s_scales[:, S : 2 * S],
+                        start=True,
+                        stop=True,
+                    )
+                nc.vector.tensor_copy(out=scores_b[:, 2 * h : 2 * h + 2, :], in_=score_ps[:])
+
+            nc.sync.dma_start(out=out[b].rearrange("h (i p) k -> p (h i) k", p=P), in_=scores_b[:])

@@ -19,6 +19,7 @@ ROWS = 2 * S
 ROW_TILES = ROWS // P
 CHUNKS = D // P
 GAMMA = 64.0
+RUN = 4
 
 FLOPS = 2 * (2 * B * H * S * D * D) + 2 * B * H * S * S * D
 
@@ -132,17 +133,21 @@ def tile_decoder_pb_t_e_kernel(tc, hq1, hk1, proj1_words, proj1_scales, bias1, o
                         op1=ALU.add,
                     )
 
-                z_by_column = z[:].rearrange("p m s -> p s m")
-                magnitude = work.tile([P, ROWS, CHUNKS], F32, name="magnitude")
-                nc.scalar.activation(out=magnitude[:], in_=z_by_column, func=ACT.Abs)
-                rsqrt = work.tile([P, ROWS, CHUNKS], F32, name="rsqrt")
+                magnitude = work.tile([P, CHUNKS, ROWS], F32, name="magnitude")
+                nc.scalar.activation(out=magnitude[:], in_=z[:], func=ACT.Abs)
+                rsqrt = work.tile([P, CHUNKS, ROWS], F32, name="rsqrt")
                 nc.scalar.activation(
                     out=rsqrt[:], in_=magnitude[:], func=ACT.Abs_reciprocal_sqrt, bias=inv_gamma[:, 0:1], scale=1.0
                 )
-                recip = work.tile([P, ROWS, CHUNKS], F32, name="recip")
+                recip = work.tile([P, CHUNKS, ROWS], F32, name="recip")
                 nc.scalar.activation(out=recip[:], in_=rsqrt[:], func=ACT.Square)
                 squashed = work.tile([P, ROWS, CHUNKS], BF16, name="squashed", align_bytes=64)
-                nc.vector.tensor_tensor(out=squashed[:], in0=z_by_column, in1=recip[:], op=ALU.mult)
+                nc.vector.tensor_tensor(
+                    out=squashed[:].rearrange("p (c i) m -> p c m i", i=RUN),
+                    in0=z[:].rearrange("p m (c i) -> p c m i", i=RUN),
+                    in1=recip[:].rearrange("p m (c i) -> p c m i", i=RUN),
+                    op=ALU.mult,
+                )
 
                 s_codes = work.tile([P, ROWS], U32, name="s_codes", align_bytes=64)
                 s_scales = work.tile([P, ROWS], U8, name="s_scales", align_bytes=64)

@@ -20,6 +20,7 @@ ROW_TILES = ROWS // P
 CHUNKS = D // P
 GAMMA = 64.0
 RUN = 4
+ROUNDS = B * H
 
 FLOPS = 2 * (2 * B * H * S * D * D) + 2 * B * H * S * S * D
 
@@ -64,110 +65,172 @@ def tile_decoder_pb_t_e_kernel(tc, hq1, hk1, proj1_words, proj1_scales, bias1, o
 
         loads = ctx.enter_context(tc.tile_pool(name="loads", bufs=3))
         work = ctx.enter_context(tc.tile_pool(name="work", bufs=2))
-        stores = ctx.enter_context(tc.tile_pool(name="stores", bufs=2))
         words_psum = ctx.enter_context(tc.psum_pool(name="words_psum", bufs=2))
         plain_psum = ctx.enter_context(tc.psum_pool(name="plain_psum", bufs=2))
         proj_psum = ctx.enter_context(tc.psum_pool(name="proj_psum", bufs=3))
         score_psum = ctx.enter_context(tc.psum_pool(name="score_psum", bufs=1))
 
-        for b in range(B):
-            xq_b = loads.tile([P, H * S // P, D], BF16, name="xq_b")
-            nc.sync.dma_start(out=xq_b[:], in_=hq1[b].rearrange("h (i p) d -> p (h i) d", p=P))
-            xk_b = loads.tile([P, H * S // P, D], BF16, name="xk_b")
-            nc.sync.dma_start(out=xk_b[:], in_=hk1[b].rearrange("h (i p) d -> p (h i) d", p=P))
-            scores_b = stores.tile([P, H * S // P, S], F32, name="scores_b")
+        live = {}
 
-            for h in range(H):
-                row_tiles = [xq_b[:, 2 * h, :], xq_b[:, 2 * h + 1, :], xk_b[:, 2 * h, :], xk_b[:, 2 * h + 1, :]]
+        def load_batch(b):
+            for name, source in (("xq", hq1), ("xk", hk1)):
+                live[name, b] = loads.tile([P, H * S // P, D], BF16, name=name)
+                nc.sync.dma_start(out=live[name, b][:], in_=source[b].rearrange("h (i p) d -> p (h i) d", p=P))
 
-                x_grouped = work.tile([P, ROWS * PACK], BF16, name="x_grouped", align_bytes=64)
-                x_grouped_words = x_grouped[:].bitcast(F32).rearrange("p (s u) -> p s u", u=2)
-                for half in range(2):
-                    words_ps = words_psum.tile([P, 2, S], F32, name="words_ps")
-                    for i in range(2):
-                        words = row_tiles[2 * half + i].bitcast(F32)
-                        for u in range(2):
-                            nc.tensor.transpose(
-                                words_ps[:, u, P * i : P * (i + 1)], words[:, u : D // 2 : 2], ident_f32[:]
-                            )
-                    nc.vector.tensor_copy(
-                        out=x_grouped_words[:, S * half : S * (half + 1), :],
-                        in_=words_ps[:].rearrange("p u s -> p s u"),
-                    )
+        def row_tiles(r):
+            b, h = divmod(r, H)
+            xq, xk = live["xq", b], live["xk", b]
+            return [xq[:, 2 * h, :], xq[:, 2 * h + 1, :], xk[:, 2 * h, :], xk[:, 2 * h + 1, :]]
 
-                x_plain = work.tile([P, CHUNKS, ROWS], BF16, name="x_plain")
-                for pair in range(2):
-                    plain_ps = plain_psum.tile([P, 2, ROWS], BF16, name="plain_ps")
-                    for mm in range(2):
-                        m = 2 * pair + mm
-                        for r in range(ROW_TILES):
-                            nc.tensor.transpose(
-                                plain_ps[:, mm, P * r : P * (r + 1)],
-                                row_tiles[r][:, P * m : P * (m + 1)],
-                                ident_bf16[:],
-                            )
-                    nc.scalar.copy(out=x_plain[:, 2 * pair : 2 * pair + 2, :], in_=plain_ps[:])
+        def transpose_words(r):
+            for half in range(2):
+                words_ps = words_psum.tile([P, 2, S], F32, name="words_ps")
+                live["words_ps", r, half] = words_ps
+                for i in range(2):
+                    words = row_tiles(r)[2 * half + i].bitcast(F32)
+                    for u in range(2):
+                        nc.tensor.transpose(words_ps[:, u, P * i : P * (i + 1)], words[:, u : D // 2 : 2], ident_f32[:])
 
-                x_codes = work.tile([P, ROWS], U32, name="x_codes", align_bytes=64)
-                x_scales = work.tile([P, ROWS], U8, name="x_scales", align_bytes=64)
-                nc.vector.quantize_mx(out=x_codes[:].bitcast(FP8X4), scales=x_scales[:], in_=x_grouped[:])
+        def copy_words(r, half):
+            if half == 0:
+                live["x_grouped", r] = work.tile([P, ROWS * PACK], BF16, name="x_grouped", align_bytes=64)
+            grouped_words = live["x_grouped", r][:].bitcast(F32).rearrange("p (s u) -> p s u", u=2)
+            nc.vector.tensor_copy(
+                out=grouped_words[:, S * half : S * (half + 1), :],
+                in_=live["words_ps", r, half][:].rearrange("p u s -> p s u"),
+            )
 
-                z = work.tile([P, CHUNKS, ROWS], F32, name="z")
-                for m in range(CHUNKS):
-                    proj_ps = proj_psum.tile([P, ROWS], F32, name="proj_ps")
-                    nc.tensor.matmul_mx(
-                        out=proj_ps[:],
-                        lhsT=w_words[:, h, P * PACK * m : P * PACK * (m + 1)].bitcast(FP8X4),
-                        lhsT_scale=w_scales[:, h, P * m : P * (m + 1)],
-                        rhs=x_codes[:].bitcast(FP8X4),
-                        rhs_scale=x_scales[:],
-                        start=True,
-                        stop=True,
-                    )
-                    nc.vector.scalar_tensor_tensor(
-                        out=z[:, m, :],
-                        in0=proj_ps[:],
-                        scalar=bias_col[:, CHUNKS * h + m : CHUNKS * h + m + 1],
-                        in1=x_plain[:, m, :],
-                        op0=ALU.add,
-                        op1=ALU.add,
-                    )
+        def transpose_plain(r):
+            for pair in range(2):
+                plain_ps = plain_psum.tile([P, 2, ROWS], BF16, name="plain_ps")
+                live["plain_ps", r, pair] = plain_ps
+                for mm in range(2):
+                    m = 2 * pair + mm
+                    for t in range(ROW_TILES):
+                        nc.tensor.transpose(
+                            plain_ps[:, mm, P * t : P * (t + 1)], row_tiles(r)[t][:, P * m : P * (m + 1)], ident_bf16[:]
+                        )
 
-                magnitude = work.tile([P, CHUNKS, ROWS], F32, name="magnitude")
-                nc.scalar.activation(out=magnitude[:], in_=z[:], func=ACT.Abs)
-                rsqrt = work.tile([P, CHUNKS, ROWS], F32, name="rsqrt")
+        def copy_plain(r):
+            live["x_plain", r] = work.tile([P, CHUNKS, ROWS], BF16, name="x_plain")
+            for pair in range(2):
+                nc.scalar.copy(out=live["x_plain", r][:, 2 * pair : 2 * pair + 2, :], in_=live["plain_ps", r, pair][:])
+
+        def quantise_x(r):
+            live["x_codes", r] = work.tile([P, ROWS], U32, name="x_codes", align_bytes=64)
+            live["x_scales", r] = work.tile([P, ROWS], U8, name="x_scales", align_bytes=64)
+            nc.vector.quantize_mx(
+                out=live["x_codes", r][:].bitcast(FP8X4), scales=live["x_scales", r][:], in_=live["x_grouped", r][:]
+            )
+
+        def project(r, m):
+            h = r % H
+            live["proj_ps", r, m] = proj_psum.tile([P, ROWS], F32, name="proj_ps")
+            nc.tensor.matmul_mx(
+                out=live["proj_ps", r, m][:],
+                lhsT=w_words[:, h, P * PACK * m : P * PACK * (m + 1)].bitcast(FP8X4),
+                lhsT_scale=w_scales[:, h, P * m : P * (m + 1)],
+                rhs=live["x_codes", r][:].bitcast(FP8X4),
+                rhs_scale=live["x_scales", r][:],
+                start=True,
+                stop=True,
+            )
+
+        def add_bias_and_residual(r, m):
+            h = r % H
+            if m == 0:
+                live["z", r] = work.tile([P, CHUNKS, ROWS], F32, name="z", bufs=3)
+            nc.vector.scalar_tensor_tensor(
+                out=live["z", r][:, m, :],
+                in0=live["proj_ps", r, m][:],
+                scalar=bias_col[:, CHUNKS * h + m : CHUNKS * h + m + 1],
+                in1=live["x_plain", r][:, m, :],
+                op0=ALU.add,
+                op1=ALU.add,
+            )
+
+        def reciprocal_of_denominator(r):
+            magnitude = work.tile([P, CHUNKS, ROWS], F32, name="magnitude")
+            rsqrt = work.tile([P, CHUNKS, ROWS], F32, name="rsqrt")
+            recip = work.tile([P, CHUNKS, ROWS], F32, name="recip")
+            live["recip", r] = recip
+            halves = (slice(0, 2), slice(2, 4))
+            for g in halves:
+                nc.scalar.activation(out=magnitude[:, g, :], in_=live["z", r][:, g, :], func=ACT.Abs)
+            for g in halves:
                 nc.scalar.activation(
-                    out=rsqrt[:], in_=magnitude[:], func=ACT.Abs_reciprocal_sqrt, bias=inv_gamma[:, 0:1], scale=1.0
+                    out=rsqrt[:, g, :],
+                    in_=magnitude[:, g, :],
+                    func=ACT.Abs_reciprocal_sqrt,
+                    bias=inv_gamma[:, 0:1],
+                    scale=1.0,
                 )
-                recip = work.tile([P, CHUNKS, ROWS], F32, name="recip")
-                nc.scalar.activation(out=recip[:], in_=rsqrt[:], func=ACT.Square)
-                squashed = work.tile([P, ROWS, CHUNKS], BF16, name="squashed", align_bytes=64)
-                nc.vector.tensor_tensor(
-                    out=squashed[:].rearrange("p (c i) m -> p c m i", i=RUN),
-                    in0=z[:].rearrange("p m (c i) -> p c m i", i=RUN),
-                    in1=recip[:].rearrange("p m (c i) -> p c m i", i=RUN),
-                    op=ALU.mult,
+            for g in halves:
+                nc.scalar.activation(out=recip[:, g, :], in_=rsqrt[:, g, :], func=ACT.Square)
+
+        def multiply_and_regroup(r):
+            live["squashed", r] = work.tile([P, ROWS, CHUNKS], BF16, name="squashed", align_bytes=64)
+            nc.vector.tensor_tensor(
+                out=live["squashed", r][:].rearrange("p (c i) m -> p c m i", i=RUN),
+                in0=live["z", r][:].rearrange("p m (c i) -> p c m i", i=RUN),
+                in1=live["recip", r][:].rearrange("p m (c i) -> p c m i", i=RUN),
+                op=ALU.mult,
+            )
+
+        def quantise_squashed(r):
+            live["s_codes", r] = work.tile([P, ROWS], U32, name="s_codes", align_bytes=64)
+            live["s_scales", r] = work.tile([P, ROWS], U8, name="s_scales", align_bytes=64)
+            nc.vector.quantize_mx(
+                out=live["s_codes", r][:].bitcast(FP8X4),
+                scales=live["s_scales", r][:],
+                in_=live["squashed", r][:].rearrange("p s m -> p (s m)"),
+            )
+
+        def scores(r):
+            codes, scales = live["s_codes", r], live["s_scales", r]
+            live["score_ps", r] = score_psum.tile([P, S // P, S], F32, name="score_ps")
+            for i in range(S // P):
+                nc.tensor.matmul_mx(
+                    out=live["score_ps", r][:, i, :],
+                    lhsT=codes[:, P * i : P * (i + 1)].bitcast(FP8X4),
+                    lhsT_scale=scales[:, P * i : P * (i + 1)],
+                    rhs=codes[:, S : 2 * S].bitcast(FP8X4),
+                    rhs_scale=scales[:, S : 2 * S],
+                    start=True,
+                    stop=True,
                 )
 
-                s_codes = work.tile([P, ROWS], U32, name="s_codes", align_bytes=64)
-                s_scales = work.tile([P, ROWS], U8, name="s_scales", align_bytes=64)
-                nc.vector.quantize_mx(
-                    out=s_codes[:].bitcast(FP8X4),
-                    scales=s_scales[:],
-                    in_=squashed[:].rearrange("p s m -> p (s m)"),
-                )
+        def copy_and_store_scores(r):
+            b, h = divmod(r, H)
+            if h == 0:
+                live["scores", b] = work.tile([P, H * S // P, S], F32, name="scores")
+            nc.vector.tensor_copy(out=live["scores", b][:, 2 * h : 2 * h + 2, :], in_=live["score_ps", r][:])
+            if h == H - 1:
+                nc.sync.dma_start(out=out[b].rearrange("h (i p) k -> p (h i) k", p=P), in_=live["scores", b][:])
 
-                score_ps = score_psum.tile([P, S // P, S], F32, name="score_ps")
-                for i in range(S // P):
-                    nc.tensor.matmul_mx(
-                        out=score_ps[:, i, :],
-                        lhsT=s_codes[:, P * i : P * (i + 1)].bitcast(FP8X4),
-                        lhsT_scale=s_scales[:, P * i : P * (i + 1)],
-                        rhs=s_codes[:, S : 2 * S].bitcast(FP8X4),
-                        rhs_scale=s_scales[:, S : 2 * S],
-                        start=True,
-                        stop=True,
-                    )
-                nc.vector.tensor_copy(out=scores_b[:, 2 * h : 2 * h + 2, :], in_=score_ps[:])
+        def when_valid(stage, r, *part):
+            if 0 <= r < ROUNDS:
+                stage(r, *part)
 
-            nc.sync.dma_start(out=out[b].rearrange("h (i p) k -> p (h i) k", p=P), in_=scores_b[:])
+        with tc.manual_schedule():
+            for i in range(-4, ROUNDS + 2):
+                if (i + 4) % H == 0 and i + 4 < ROUNDS:
+                    load_batch((i + 4) // H)
+                when_valid(add_bias_and_residual, i, 0)
+                when_valid(project, i, 3)
+                when_valid(transpose_words, i + 2)
+                when_valid(copy_plain, i + 1)
+                when_valid(transpose_plain, i + 2)
+                when_valid(add_bias_and_residual, i, 1)
+                when_valid(copy_and_store_scores, i - 2)
+                when_valid(add_bias_and_residual, i, 2)
+                when_valid(add_bias_and_residual, i, 3)
+                when_valid(reciprocal_of_denominator, i)
+                when_valid(multiply_and_regroup, i - 1)
+                when_valid(quantise_x, i + 1)
+                for m in range(3):
+                    when_valid(project, i + 1, m)
+                when_valid(copy_words, i + 2, 0)
+                when_valid(quantise_squashed, i - 1)
+                when_valid(scores, i - 1)
+                when_valid(copy_words, i + 2, 1)

@@ -165,8 +165,9 @@ def tile_decoder_pb_t_e_kernel(tc, hq1, hk1, proj1_words, proj1_scales, bias1, o
                     bias=inv_gamma[:, 0:1],
                     scale=1.0,
                 )
-            for g in halves:
-                nc.scalar.activation(out=recip[:, g, :], in_=rsqrt[:, g, :], func=ACT.Square)
+            nc.scalar.activation(out=recip[:, halves[0], :], in_=rsqrt[:, halves[0], :], func=ACT.Square)
+            for m in (2, 3):
+                nc.gpsimd.tensor_tensor(out=recip[:, m, :], in0=rsqrt[:, m, :], in1=rsqrt[:, m, :], op=ALU.mult)
 
         def multiply_and_regroup(r):
             live["squashed", r] = work.tile([P, ROWS, CHUNKS], BF16, name="squashed", align_bytes=64)
@@ -204,7 +205,7 @@ def tile_decoder_pb_t_e_kernel(tc, hq1, hk1, proj1_words, proj1_scales, bias1, o
             b, h = divmod(r, H)
             if h == 0:
                 live["scores", b] = work.tile([P, H * S // P, S], F32, name="scores")
-            nc.vector.tensor_copy(out=live["scores", b][:, 2 * h : 2 * h + 2, :], in_=live["score_ps", r][:])
+            nc.scalar.copy(out=live["scores", b][:, 2 * h : 2 * h + 2, :], in_=live["score_ps", r][:])
             if h == H - 1:
                 nc.sync.dma_start(out=out[b].rearrange("h (i p) k -> p (h i) k", p=P), in_=live["scores", b][:])
 
@@ -221,16 +222,15 @@ def tile_decoder_pb_t_e_kernel(tc, hq1, hk1, proj1_words, proj1_scales, bias1, o
                 when_valid(transpose_words, i + 2)
                 when_valid(copy_plain, i + 1)
                 when_valid(transpose_plain, i + 2)
-                when_valid(add_bias_and_residual, i, 1)
                 when_valid(copy_and_store_scores, i - 2)
-                when_valid(add_bias_and_residual, i, 2)
-                when_valid(add_bias_and_residual, i, 3)
+                for m in range(1, CHUNKS):
+                    when_valid(add_bias_and_residual, i, m)
                 when_valid(reciprocal_of_denominator, i)
                 when_valid(multiply_and_regroup, i - 1)
                 when_valid(quantise_x, i + 1)
                 for m in range(3):
                     when_valid(project, i + 1, m)
-                when_valid(copy_words, i + 2, 0)
                 when_valid(quantise_squashed, i - 1)
                 when_valid(scores, i - 1)
-                when_valid(copy_words, i + 2, 1)
+                for half in range(2):
+                    when_valid(copy_words, i + 2, half)

@@ -15,12 +15,13 @@ ALU = mybir.AluOpType
 P = 128
 PACK = 4
 B, H, S, D = 16, 2, 256, 512
+ROUNDS = B * H
 ROWS = 2 * S
 ROW_TILES = ROWS // P
 CHUNKS = D // P
 GAMMA = 64.0
 RUN = 4
-ROUNDS = B * H
+LOAD_AHEAD = 4
 
 FLOPS = 2 * (2 * B * H * S * D * D) + 2 * B * H * S * S * D
 
@@ -29,65 +30,59 @@ def tile_decoder_pb_t_e_kernel(tc, hq1, hk1, proj1_words, proj1_scales, bias1, o
     nc = tc.nc
     with ExitStack() as ctx:
         const = ctx.enter_context(tc.tile_pool(name="const", bufs=1))
-
-        ident_f32 = const.tile([P, P], F32, name="ident_f32")
-        masks.make_identity(nc, ident_f32[:])
-        ident_bf16 = const.tile([P, P], BF16, name="ident_bf16")
-        masks.make_identity(nc, ident_bf16[:])
-        inv_gamma = const.tile([P, 1], F32, name="inv_gamma")
-        nc.vector.memset(inv_gamma[:], 1.0 / GAMMA)
-
-        w_words = const.tile([P, H, D * PACK], U8, name="w_words", align_bytes=64)
-        for h in range(H):
-            nc.sync.dma_start(
-                out=w_words[:, h, :].bitcast(I32),
-                in_=proj1_words[h].rearrange("p n t -> p (n t)").bitcast(I32),
-            )
-        w_scales = const.tile([P, H, D], U8, name="w_scales", align_bytes=64)
-        nc.vector.memset(w_scales[:].rearrange("p h n -> p (h n)").bitcast(I32), 0)
-        for quadrant in range(4):
-            nc.sync.dma_start(
-                out=w_scales[32 * quadrant : 32 * quadrant + 4, :, :].bitcast(I32),
-                in_=proj1_scales[:, 4 * quadrant : 4 * quadrant + 4, :].rearrange("h r n -> r h n").bitcast(I32),
-            )
-
-        bias_rows = const.tile([P, P], BF16, name="bias_rows")
-        nc.vector.memset(bias_rows[:], 0.0)
-        nc.sync.dma_start(
-            out=bias_rows[0 : H * CHUNKS, :],
-            in_=bias1.rearrange("a h c (m j) -> (a h c m) j", j=P),
-        )
-        bias_col = const.tile([P, H * CHUNKS], F32, name="bias_col")
-        with tc.psum_pool(name="setup_psum", bufs=1) as setup_psum:
-            bias_ps = setup_psum.tile([P, P], BF16, name="bias_ps")
-            nc.tensor.transpose(bias_ps[:], bias_rows[:], ident_bf16[:])
-            nc.vector.tensor_copy(out=bias_col[:], in_=bias_ps[:, 0 : H * CHUNKS])
-
-        loads = ctx.enter_context(tc.tile_pool(name="loads", bufs=3))
+        loads = ctx.enter_context(tc.tile_pool(name="loads", bufs=LOAD_AHEAD))
         work = ctx.enter_context(tc.tile_pool(name="work", bufs=2))
         words_psum = ctx.enter_context(tc.psum_pool(name="words_psum", bufs=2))
         plain_psum = ctx.enter_context(tc.psum_pool(name="plain_psum", bufs=2))
         proj_psum = ctx.enter_context(tc.psum_pool(name="proj_psum", bufs=3))
         score_psum = ctx.enter_context(tc.psum_pool(name="score_psum", bufs=1))
 
+        ident_f32 = const.tile([P, P], F32, name="ident_f32")
+        ident_bf16 = const.tile([P, P], BF16, name="ident_bf16")
+        inv_gamma = const.tile([P, 1], F32, name="inv_gamma")
+        w_words = const.tile([P, H, D * PACK], U8, name="w_words", align_bytes=64)
+        w_scales = const.tile([P, H, D], U8, name="w_scales", align_bytes=64)
+        bias_rows = const.tile([P, P], BF16, name="bias_rows")
+        bias_col = const.tile([P, H * CHUNKS], F32, name="bias_col")
+
         live = {}
 
-        def load_batch(b):
-            for name, source in (("xq", hq1), ("xk", hk1)):
-                live[name, b] = loads.tile([P, H * S // P, D], BF16, name=name)
-                nc.sync.dma_start(out=live[name, b][:], in_=source[b].rearrange("h (i p) d -> p (h i) d", p=P))
+        def load_constants():
+            masks.make_identity(nc, ident_f32[:])
+            masks.make_identity(nc, ident_bf16[:])
+            nc.vector.memset(inv_gamma[:], 1.0 / GAMMA)
 
-        def row_tiles(r):
+            nc.vector.memset(bias_rows[:], 0.0)
+            nc.sync.dma_start(out=bias_rows[0 : H * CHUNKS, :], in_=bias1.rearrange("a h c (m j) -> (a h c m) j", j=P))
+
+            nc.vector.memset(w_scales[:].rearrange("p h n -> p (h n)").bitcast(I32), 0)
+            for quadrant in range(4):
+                nc.sync.dma_start(
+                    out=w_scales[32 * quadrant : 32 * quadrant + 4, :, :].bitcast(I32),
+                    in_=proj1_scales[:, 4 * quadrant : 4 * quadrant + 4, :].rearrange("h r n -> r h n").bitcast(I32),
+                )
+            for h in range(H):
+                nc.sync.dma_start(
+                    out=w_words[:, h, :].bitcast(I32),
+                    in_=proj1_words[h].rearrange("p n t -> p (n t)").bitcast(I32),
+                )
+
+            bias_ps = plain_psum.tile([P, 2, ROWS], BF16, name="plain_ps")
+            nc.tensor.transpose(bias_ps[:, 0, 0:P], bias_rows[:], ident_bf16[:])
+            nc.vector.tensor_copy(out=bias_col[:], in_=bias_ps[:, 0, 0 : H * CHUNKS])
+
+        def load_rows(r):
             b, h = divmod(r, H)
-            xq, xk = live["xq", b], live["xk", b]
-            return [xq[:, 2 * h, :], xq[:, 2 * h + 1, :], xk[:, 2 * h, :], xk[:, 2 * h + 1, :]]
+            live["x", r] = loads.tile([P, ROW_TILES, D], BF16, name="x")
+            nc.sync.dma_start(out=live["x", r][:, 0:2, :], in_=hq1[b, h].rearrange("(t p) d -> p t d", p=P))
+            nc.sync.dma_start(out=live["x", r][:, 2:4, :], in_=hk1[b, h].rearrange("(t p) d -> p t d", p=P))
 
         def transpose_words(r):
             for half in range(2):
                 words_ps = words_psum.tile([P, 2, S], F32, name="words_ps")
                 live["words_ps", r, half] = words_ps
                 for i in range(2):
-                    words = row_tiles(r)[2 * half + i].bitcast(F32)
+                    words = live["x", r][:, 2 * half + i, :].bitcast(F32)
                     for u in range(2):
                         nc.tensor.transpose(words_ps[:, u, P * i : P * (i + 1)], words[:, u : D // 2 : 2], ident_f32[:])
 
@@ -108,7 +103,7 @@ def tile_decoder_pb_t_e_kernel(tc, hq1, hk1, proj1_words, proj1_scales, bias1, o
                     m = 2 * pair + mm
                     for t in range(ROW_TILES):
                         nc.tensor.transpose(
-                            plain_ps[:, mm, P * t : P * (t + 1)], row_tiles(r)[t][:, P * m : P * (m + 1)], ident_bf16[:]
+                            plain_ps[:, mm, P * t : P * (t + 1)], live["x", r][:, t, P * m : P * (m + 1)], ident_bf16[:]
                         )
 
         def copy_plain(r):
@@ -190,11 +185,11 @@ def tile_decoder_pb_t_e_kernel(tc, hq1, hk1, proj1_words, proj1_scales, bias1, o
         def scores(r):
             codes, scales = live["s_codes", r], live["s_scales", r]
             live["score_ps", r] = score_psum.tile([P, S // P, S], F32, name="score_ps")
-            for i in range(S // P):
+            for t in range(S // P):
                 nc.tensor.matmul_mx(
-                    out=live["score_ps", r][:, i, :],
-                    lhsT=codes[:, P * i : P * (i + 1)].bitcast(FP8X4),
-                    lhsT_scale=scales[:, P * i : P * (i + 1)],
+                    out=live["score_ps", r][:, t, :],
+                    lhsT=codes[:, P * t : P * (t + 1)].bitcast(FP8X4),
+                    lhsT_scale=scales[:, P * t : P * (t + 1)],
                     rhs=codes[:, S : 2 * S].bitcast(FP8X4),
                     rhs_scale=scales[:, S : 2 * S],
                     start=True,
@@ -203,20 +198,19 @@ def tile_decoder_pb_t_e_kernel(tc, hq1, hk1, proj1_words, proj1_scales, bias1, o
 
         def copy_and_store_scores(r):
             b, h = divmod(r, H)
-            if h == 0:
-                live["scores", b] = work.tile([P, H * S // P, S], F32, name="scores")
-            nc.scalar.copy(out=live["scores", b][:, 2 * h : 2 * h + 2, :], in_=live["score_ps", r][:])
-            if h == H - 1:
-                nc.sync.dma_start(out=out[b].rearrange("h (i p) k -> p (h i) k", p=P), in_=live["scores", b][:])
+            result = work.tile([P, S // P, S], F32, name="result")
+            nc.scalar.copy(out=result[:], in_=live["score_ps", r][:])
+            nc.sync.dma_start(out=out[b, h].rearrange("(t p) k -> p t k", p=P), in_=result[:])
 
         def when_valid(stage, r, *part):
             if 0 <= r < ROUNDS:
                 stage(r, *part)
 
         with tc.manual_schedule():
-            for i in range(-4, ROUNDS + 2):
-                if (i + 4) % H == 0 and i + 4 < ROUNDS:
-                    load_batch((i + 4) // H)
+            load_rows(0)
+            load_constants()
+            for i in range(1 - LOAD_AHEAD, ROUNDS + 2):
+                when_valid(load_rows, i + LOAD_AHEAD)
                 when_valid(add_bias_and_residual, i, 0)
                 when_valid(project, i, 3)
                 when_valid(transpose_words, i + 2)

@@ -32,44 +32,41 @@ def tile_decoder_pb_t_e_kernel(tc, hq1, hk1, proj1_words, proj1_scales, bias1, o
         const = ctx.enter_context(tc.tile_pool(name="const", bufs=1))
         loads = ctx.enter_context(tc.tile_pool(name="loads", bufs=LOAD_AHEAD))
         work = ctx.enter_context(tc.tile_pool(name="work", bufs=2))
-        words_psum = ctx.enter_context(tc.psum_pool(name="words_psum", bufs=2))
-        plain_psum = ctx.enter_context(tc.psum_pool(name="plain_psum", bufs=2))
-        proj_psum = ctx.enter_context(tc.psum_pool(name="proj_psum", bufs=3))
+        words_psum = ctx.enter_context(tc.psum_pool(name="words_psum", bufs=3))
+        proj_psum = ctx.enter_context(tc.psum_pool(name="proj_psum", bufs=4))
         score_psum = ctx.enter_context(tc.psum_pool(name="score_psum", bufs=1))
 
         ident_f32 = const.tile([P, P], F32, name="ident_f32")
-        ident_bf16 = const.tile([P, P], BF16, name="ident_bf16")
         inv_gamma = const.tile([P, 1], F32, name="inv_gamma")
-        w_words = const.tile([P, H, D * PACK], U8, name="w_words", align_bytes=64)
-        w_scales = const.tile([P, H, D], U8, name="w_scales", align_bytes=64)
-        bias_rows = const.tile([P, P], BF16, name="bias_rows")
+        words_raw = const.tile([P, H, D], I32, name="words_raw", align_bytes=64)
+        scales_raw = const.tile([P, H, D], U8, name="scales_raw", align_bytes=64)
+        w_words = const.tile([P, H, CHUNKS, P], I32, name="w_words", align_bytes=64)
+        w_scales = const.tile([P, H, CHUNKS, P], U8, name="w_scales", align_bytes=64)
+        bias_bf16 = const.tile([P, H, CHUNKS], BF16, name="bias_bf16")
         bias_col = const.tile([P, H * CHUNKS], F32, name="bias_col")
 
         live = {}
 
         def load_constants():
             masks.make_identity(nc, ident_f32[:])
-            masks.make_identity(nc, ident_bf16[:])
             nc.vector.memset(inv_gamma[:], 1.0 / GAMMA)
 
-            nc.vector.memset(bias_rows[:], 0.0)
-            nc.sync.dma_start(out=bias_rows[0 : H * CHUNKS, :], in_=bias1.rearrange("a h c (m j) -> (a h c m) j", j=P))
-
-            nc.vector.memset(w_scales[:].rearrange("p h n -> p (h n)").bitcast(I32), 0)
+            nc.vector.memset(scales_raw[:].rearrange("p h n -> p (h n)").bitcast(I32), 0)
             for quadrant in range(4):
                 nc.sync.dma_start(
-                    out=w_scales[32 * quadrant : 32 * quadrant + 4, :, :].bitcast(I32),
+                    out=scales_raw[32 * quadrant : 32 * quadrant + 4, :, :].bitcast(I32),
                     in_=proj1_scales[:, 4 * quadrant : 4 * quadrant + 4, :].rearrange("h r n -> r h n").bitcast(I32),
                 )
             for h in range(H):
                 nc.sync.dma_start(
-                    out=w_words[:, h, :].bitcast(I32),
-                    in_=proj1_words[h].rearrange("p n t -> p (n t)").bitcast(I32),
+                    out=words_raw[:, h, :], in_=proj1_words[h].rearrange("p n t -> p (n t)").bitcast(I32)
                 )
+            nc.sync.dma_start(out=bias_bf16[:], in_=bias1.rearrange("a h c (j m) -> j (a h c) m", m=CHUNKS))
+            nc.vector.tensor_copy(out=bias_col[:], in_=bias_bf16[:].rearrange("p h m -> p (h m)"))
 
-            bias_ps = plain_psum.tile([P, 2, ROWS], BF16, name="plain_ps")
-            nc.tensor.transpose(bias_ps[:, 0, 0:P], bias_rows[:], ident_bf16[:])
-            nc.vector.tensor_copy(out=bias_col[:], in_=bias_ps[:, 0, 0 : H * CHUNKS])
+            for h in range(H):
+                nc.vector.tensor_copy(out=w_words[:, h], in_=words_raw[:, h, :].rearrange("p (j m) -> p m j", m=CHUNKS))
+                nc.vector.tensor_copy(out=w_scales[:, h], in_=scales_raw[:, h, :].rearrange("p (j m) -> p m j", m=CHUNKS))
 
         def load_rows(r):
             b, h = divmod(r, H)
@@ -88,28 +85,12 @@ def tile_decoder_pb_t_e_kernel(tc, hq1, hk1, proj1_words, proj1_scales, bias1, o
 
         def copy_words(r, half):
             if half == 0:
-                live["x_grouped", r] = work.tile([P, ROWS * PACK], BF16, name="x_grouped", align_bytes=64)
+                live["x_grouped", r] = work.tile([P, ROWS * PACK], BF16, name="x_grouped", align_bytes=64, bufs=3)
             grouped_words = live["x_grouped", r][:].bitcast(F32).rearrange("p (s u) -> p s u", u=2)
             nc.vector.tensor_copy(
                 out=grouped_words[:, S * half : S * (half + 1), :],
                 in_=live["words_ps", r, half][:].rearrange("p u s -> p s u"),
             )
-
-        def transpose_plain(r):
-            for pair in range(2):
-                plain_ps = plain_psum.tile([P, 2, ROWS], BF16, name="plain_ps")
-                live["plain_ps", r, pair] = plain_ps
-                for mm in range(2):
-                    m = 2 * pair + mm
-                    for t in range(ROW_TILES):
-                        nc.tensor.transpose(
-                            plain_ps[:, mm, P * t : P * (t + 1)], live["x", r][:, t, P * m : P * (m + 1)], ident_bf16[:]
-                        )
-
-        def copy_plain(r):
-            live["x_plain", r] = work.tile([P, CHUNKS, ROWS], BF16, name="x_plain")
-            for pair in range(2):
-                nc.scalar.copy(out=live["x_plain", r][:, 2 * pair : 2 * pair + 2, :], in_=live["plain_ps", r, pair][:])
 
         def quantise_x(r):
             live["x_codes", r] = work.tile([P, ROWS], U32, name="x_codes", align_bytes=64)
@@ -123,8 +104,8 @@ def tile_decoder_pb_t_e_kernel(tc, hq1, hk1, proj1_words, proj1_scales, bias1, o
             live["proj_ps", r, m] = proj_psum.tile([P, ROWS], F32, name="proj_ps")
             nc.tensor.matmul_mx(
                 out=live["proj_ps", r, m][:],
-                lhsT=w_words[:, h, P * PACK * m : P * PACK * (m + 1)].bitcast(FP8X4),
-                lhsT_scale=w_scales[:, h, P * m : P * (m + 1)],
+                lhsT=w_words[:, h, m, :].bitcast(FP8X4),
+                lhsT_scale=w_scales[:, h, m, :],
                 rhs=live["x_codes", r][:].bitcast(FP8X4),
                 rhs_scale=live["x_scales", r][:],
                 start=True,
@@ -139,7 +120,7 @@ def tile_decoder_pb_t_e_kernel(tc, hq1, hk1, proj1_words, proj1_scales, bias1, o
                 out=live["z", r][:, m, :],
                 in0=live["proj_ps", r, m][:],
                 scalar=bias_col[:, CHUNKS * h + m : CHUNKS * h + m + 1],
-                in1=live["x_plain", r][:, m, :],
+                in1=live["x_grouped", r][:].rearrange("p (s m) -> p m s", m=PACK)[:, m, :],
                 op0=ALU.add,
                 op1=ALU.add,
             )
@@ -211,18 +192,14 @@ def tile_decoder_pb_t_e_kernel(tc, hq1, hk1, proj1_words, proj1_scales, bias1, o
             load_constants()
             for i in range(1 - LOAD_AHEAD, ROUNDS + 2):
                 when_valid(load_rows, i + LOAD_AHEAD)
-                when_valid(add_bias_and_residual, i, 0)
-                when_valid(project, i, 3)
                 when_valid(transpose_words, i + 2)
-                when_valid(copy_plain, i + 1)
-                when_valid(transpose_plain, i + 2)
                 when_valid(copy_and_store_scores, i - 2)
-                for m in range(1, CHUNKS):
+                for m in range(CHUNKS):
                     when_valid(add_bias_and_residual, i, m)
                 when_valid(reciprocal_of_denominator, i)
                 when_valid(multiply_and_regroup, i - 1)
                 when_valid(quantise_x, i + 1)
-                for m in range(3):
+                for m in range(CHUNKS):
                     when_valid(project, i + 1, m)
                 when_valid(quantise_squashed, i - 1)
                 when_valid(scores, i - 1)

@@ -84,10 +84,11 @@ def tile_decoder_pb_t_e_kernel(tc, hq1, hk1, proj1_words, proj1_scales, bias1, o
                         nc.tensor.transpose(words_ps[:, u, P * i : P * (i + 1)], words[:, u : D // 2 : 2], ident_f32[:])
 
         def copy_words(r, half):
-            if half == 0:
+            if half == 1:
                 live["x_grouped", r] = work.tile([P, ROWS * PACK], BF16, name="x_grouped", align_bytes=64, bufs=3)
             grouped_words = live["x_grouped", r][:].bitcast(F32).rearrange("p (s u) -> p s u", u=2)
-            nc.vector.tensor_copy(
+            copy = nc.scalar.copy if half else nc.vector.tensor_copy
+            copy(
                 out=grouped_words[:, S * half : S * (half + 1), :],
                 in_=live["words_ps", r, half][:].rearrange("p u s -> p s u"),
             )
@@ -194,6 +195,7 @@ def tile_decoder_pb_t_e_kernel(tc, hq1, hk1, proj1_words, proj1_scales, bias1, o
                 when_valid(load_rows, i + LOAD_AHEAD)
                 when_valid(transpose_words, i + 2)
                 when_valid(copy_and_store_scores, i - 2)
+                when_valid(copy_words, i + 2, 1)
                 for m in range(CHUNKS):
                     when_valid(add_bias_and_residual, i, m)
                 when_valid(reciprocal_of_denominator, i)
@@ -203,5 +205,4 @@ def tile_decoder_pb_t_e_kernel(tc, hq1, hk1, proj1_words, proj1_scales, bias1, o
                     when_valid(project, i + 1, m)
                 when_valid(quantise_squashed, i - 1)
                 when_valid(scores, i - 1)
-                for half in range(2):
-                    when_valid(copy_words, i + 2, half)
+                when_valid(copy_words, i + 2, 0)

@@ -84,7 +84,7 @@ def tile_decoder_pb_t_e_kernel(tc, hq1, hk1, proj1_words, proj1_scales, bias1, o
                         nc.tensor.transpose(words_ps[:, u, P * i : P * (i + 1)], words[:, u : D // 2 : 2], ident_f32[:])
 
         def copy_words(r, half):
-            if half == 1:
+            if half == 0:
                 live["x_grouped", r] = work.tile([P, ROWS * PACK], BF16, name="x_grouped", align_bytes=64, bufs=3)
             grouped_words = live["x_grouped", r][:].bitcast(F32).rearrange("p (s u) -> p s u", u=2)
             copy = nc.scalar.copy if half else nc.vector.tensor_copy
@@ -129,7 +129,7 @@ def tile_decoder_pb_t_e_kernel(tc, hq1, hk1, proj1_words, proj1_scales, bias1, o
         def reciprocal_of_denominator(r):
             magnitude = work.tile([P, CHUNKS, ROWS], F32, name="magnitude")
             rsqrt = work.tile([P, CHUNKS, ROWS], F32, name="rsqrt")
-            recip = work.tile([P, CHUNKS, ROWS], F32, name="recip")
+            recip = work.tile([P, CHUNKS, ROWS], F32, name="recip", bufs=3)
             live["recip", r] = recip
             halves = (slice(0, 2), slice(2, 4))
             for g in halves:
@@ -191,18 +191,18 @@ def tile_decoder_pb_t_e_kernel(tc, hq1, hk1, proj1_words, proj1_scales, bias1, o
         with tc.manual_schedule():
             load_rows(0)
             load_constants()
-            for i in range(1 - LOAD_AHEAD, ROUNDS + 2):
+            for i in range(1 - LOAD_AHEAD, ROUNDS + 3):
                 when_valid(load_rows, i + LOAD_AHEAD)
                 when_valid(transpose_words, i + 2)
-                when_valid(copy_and_store_scores, i - 2)
-                when_valid(copy_words, i + 2, 1)
+                when_valid(copy_and_store_scores, i - 3)
                 for m in range(CHUNKS):
                     when_valid(add_bias_and_residual, i, m)
                 when_valid(reciprocal_of_denominator, i)
-                when_valid(multiply_and_regroup, i - 1)
+                when_valid(multiply_and_regroup, i - 2)
                 when_valid(quantise_x, i + 1)
                 for m in range(CHUNKS):
                     when_valid(project, i + 1, m)
-                when_valid(quantise_squashed, i - 1)
-                when_valid(scores, i - 1)
-                when_valid(copy_words, i + 2, 0)
+                when_valid(quantise_squashed, i - 2)
+                when_valid(scores, i - 2)
+                for half in range(2):
+                    when_valid(copy_words, i + 2, half)

@@ -142,8 +142,8 @@ def tile_decoder_pb_t_e_kernel(tc, hq1, hk1, proj1_words, proj1_scales, bias1, o
                     bias=inv_gamma[:, 0:1],
                     scale=1.0,
                 )
-            nc.scalar.activation(out=recip[:, halves[0], :], in_=rsqrt[:, halves[0], :], func=ACT.Square)
-            for m in (2, 3):
+            nc.scalar.activation(out=recip[:, halves[1], :], in_=rsqrt[:, halves[1], :], func=ACT.Square)
+            for m in (0, 1):
                 nc.gpsimd.tensor_tensor(out=recip[:, m, :], in0=rsqrt[:, m, :], in1=rsqrt[:, m, :], op=ALU.mult)
 
         def multiply_and_regroup(r):
@@ -191,18 +191,18 @@ def tile_decoder_pb_t_e_kernel(tc, hq1, hk1, proj1_words, proj1_scales, bias1, o
         with tc.manual_schedule():
             load_rows(0)
             load_constants()
-            for i in range(1 - LOAD_AHEAD, ROUNDS + 3):
+            for i in range(1 - LOAD_AHEAD, ROUNDS + 1):
                 when_valid(load_rows, i + LOAD_AHEAD)
                 when_valid(transpose_words, i + 2)
-                when_valid(copy_and_store_scores, i - 3)
                 for m in range(CHUNKS):
                     when_valid(add_bias_and_residual, i, m)
                 when_valid(reciprocal_of_denominator, i)
-                when_valid(multiply_and_regroup, i - 2)
+                when_valid(multiply_and_regroup, i - 1)
                 when_valid(quantise_x, i + 1)
                 for m in range(CHUNKS):
                     when_valid(project, i + 1, m)
-                when_valid(quantise_squashed, i - 2)
-                when_valid(scores, i - 2)
+                when_valid(quantise_squashed, i - 1)
+                when_valid(scores, i - 1)
                 for half in range(2):
                     when_valid(copy_words, i + 2, half)
+                when_valid(copy_and_store_scores, i - 1)

@@ -84,7 +84,7 @@ def tile_decoder_pb_t_e_kernel(tc, hq1, hk1, proj1_words, proj1_scales, bias1, o
                         nc.tensor.transpose(words_ps[:, u, P * i : P * (i + 1)], words[:, u : D // 2 : 2], ident_f32[:])
 
         def copy_words(r, half):
-            if half == 0:
+            if half == 1:
                 live["x_grouped", r] = work.tile([P, ROWS * PACK], BF16, name="x_grouped", align_bytes=64, bufs=3)
             grouped_words = live["x_grouped", r][:].bitcast(F32).rearrange("p (s u) -> p s u", u=2)
             copy = nc.scalar.copy if half else nc.vector.tensor_copy
@@ -142,9 +142,12 @@ def tile_decoder_pb_t_e_kernel(tc, hq1, hk1, proj1_words, proj1_scales, bias1, o
                     bias=inv_gamma[:, 0:1],
                     scale=1.0,
                 )
-            nc.scalar.activation(out=recip[:, halves[1], :], in_=rsqrt[:, halves[1], :], func=ACT.Square)
+            live["rsqrt", r] = rsqrt
             for m in (0, 1):
                 nc.gpsimd.tensor_tensor(out=recip[:, m, :], in0=rsqrt[:, m, :], in1=rsqrt[:, m, :], op=ALU.mult)
+
+        def square_second_half(r):
+            nc.scalar.activation(out=live["recip", r][:, 2:4, :], in_=live["rsqrt", r][:, 2:4, :], func=ACT.Square)
 
         def multiply_and_regroup(r):
             live["squashed", r] = work.tile([P, ROWS, CHUNKS], BF16, name="squashed", align_bytes=64)
@@ -197,12 +200,13 @@ def tile_decoder_pb_t_e_kernel(tc, hq1, hk1, proj1_words, proj1_scales, bias1, o
                 for m in range(CHUNKS):
                     when_valid(add_bias_and_residual, i, m)
                 when_valid(reciprocal_of_denominator, i)
+                when_valid(copy_words, i + 2, 1)
+                when_valid(square_second_half, i)
                 when_valid(multiply_and_regroup, i - 1)
                 when_valid(quantise_x, i + 1)
                 for m in range(CHUNKS):
                     when_valid(project, i + 1, m)
                 when_valid(quantise_squashed, i - 1)
                 when_valid(scores, i - 1)
-                for half in range(2):
-                    when_valid(copy_words, i + 2, half)
+                when_valid(copy_words, i + 2, 0)
                 when_valid(copy_and_store_scores, i - 1)

@@ -20,6 +20,7 @@ ROWS = 2 * S
 ROW_TILES = ROWS // P
 CHUNKS = D // P
 GAMMA = 64.0
+GPSIMD_SHARE = 1152
 RUN = 4
 LOAD_AHEAD = 4
 
@@ -42,8 +43,7 @@ def tile_decoder_pb_t_e_kernel(tc, hq1, hk1, proj1_words, proj1_scales, bias1, o
         scales_raw = const.tile([P, H, D], U8, name="scales_raw", align_bytes=64)
         w_words = const.tile([P, H, CHUNKS, P], I32, name="w_words", align_bytes=64)
         w_scales = const.tile([P, H, CHUNKS, P], U8, name="w_scales", align_bytes=64)
-        bias_bf16 = const.tile([P, H, CHUNKS], BF16, name="bias_bf16")
-        bias_col = const.tile([P, H * CHUNKS], F32, name="bias_col")
+        bias_col = const.tile([P, H, CHUNKS], BF16, name="bias_col")
 
         live = {}
 
@@ -57,16 +57,14 @@ def tile_decoder_pb_t_e_kernel(tc, hq1, hk1, proj1_words, proj1_scales, bias1, o
                     out=scales_raw[32 * quadrant : 32 * quadrant + 4, :, :].bitcast(I32),
                     in_=proj1_scales[:, 4 * quadrant : 4 * quadrant + 4, :].rearrange("h r n -> r h n").bitcast(I32),
                 )
-            for h in range(H):
-                nc.sync.dma_start(
-                    out=words_raw[:, h, :], in_=proj1_words[h].rearrange("p n t -> p (n t)").bitcast(I32)
-                )
-            nc.sync.dma_start(out=bias_bf16[:], in_=bias1.rearrange("a h c (j m) -> j (a h c) m", m=CHUNKS))
-            nc.vector.tensor_copy(out=bias_col[:], in_=bias_bf16[:].rearrange("p h m -> p (h m)"))
+            nc.sync.dma_start(out=bias_col[:], in_=bias1.rearrange("a h c (j m) -> j (a h c) m", m=CHUNKS))
 
-            for h in range(H):
-                nc.vector.tensor_copy(out=w_words[:, h], in_=words_raw[:, h, :].rearrange("p (j m) -> p m j", m=CHUNKS))
-                nc.vector.tensor_copy(out=w_scales[:, h], in_=scales_raw[:, h, :].rearrange("p (j m) -> p m j", m=CHUNKS))
+        def load_words(h):
+            nc.sync.dma_start(out=words_raw[:, h, :], in_=proj1_words[h].rearrange("p n t -> p (n t)").bitcast(I32))
+
+        def regroup_weights(h):
+            nc.vector.tensor_copy(out=w_words[:, h], in_=words_raw[:, h, :].rearrange("p (j m) -> p m j", m=CHUNKS))
+            nc.vector.tensor_copy(out=w_scales[:, h], in_=scales_raw[:, h, :].rearrange("p (j m) -> p m j", m=CHUNKS))
 
         def load_rows(r):
             b, h = divmod(r, H)
@@ -113,58 +111,68 @@ def tile_decoder_pb_t_e_kernel(tc, hq1, hk1, proj1_words, proj1_scales, bias1, o
                 stop=True,
             )
 
-        def add_bias_and_residual(r, m):
+        def add_bias_and_residual(r, m, first=0, last=ROWS):
             h = r % H
-            if m == 0:
-                live["z", r] = work.tile([P, CHUNKS, ROWS], F32, name="z", bufs=3)
+            if m == 0 and first == 0:
+                live["z", r] = work.tile([P, CHUNKS * ROWS], F32, name="z", bufs=3)
             nc.vector.scalar_tensor_tensor(
-                out=live["z", r][:, m, :],
-                in0=live["proj_ps", r, m][:],
-                scalar=bias_col[:, CHUNKS * h + m : CHUNKS * h + m + 1],
-                in1=live["x_grouped", r][:].rearrange("p (s m) -> p m s", m=PACK)[:, m, :],
+                out=live["z", r][:, ROWS * m + first : ROWS * m + last],
+                in0=live["proj_ps", r, m][:, first:last],
+                scalar=bias_col[:, h, m : m + 1],
+                in1=live["x_grouped", r][:].rearrange("p (s m) -> p m s", m=PACK)[:, m, first:last],
                 op0=ALU.add,
                 op1=ALU.add,
             )
 
-        def reciprocal_of_denominator(r):
-            magnitude = work.tile([P, CHUNKS, ROWS], F32, name="magnitude")
-            rsqrt = work.tile([P, CHUNKS, ROWS], F32, name="rsqrt")
-            recip = work.tile([P, CHUNKS, ROWS], F32, name="recip", bufs=3)
-            live["recip", r] = recip
-            halves = (slice(0, 2), slice(2, 4))
-            for g in halves:
-                nc.scalar.activation(out=magnitude[:, g, :], in_=live["z", r][:, g, :], func=ACT.Abs)
-            for g in halves:
+        def part(r, tile, k):
+            if r == ROUNDS - 1:
+                return tile[:].rearrange("p (m s) -> p m s", m=CHUNKS)[:, :, S * k : S * (k + 1)]
+            return tile[:, GPSIMD_SHARE:] if k else tile[:, 0:GPSIMD_SHARE]
+
+        def reciprocal_roots(r):
+            magnitude = work.tile([P, CHUNKS * ROWS], F32, name="magnitude")
+            live["rsqrt", r] = work.tile([P, CHUNKS * ROWS], F32, name="rsqrt")
+            live["recip", r] = work.tile([P, CHUNKS * ROWS], F32, name="recip", bufs=3)
+            for k in range(2):
+                nc.scalar.activation(out=part(r, magnitude, k), in_=part(r, live["z", r], k), func=ACT.Abs)
+            for k in range(2):
                 nc.scalar.activation(
-                    out=rsqrt[:, g, :],
-                    in_=magnitude[:, g, :],
+                    out=part(r, live["rsqrt", r], k),
+                    in_=part(r, magnitude, k),
                     func=ACT.Abs_reciprocal_sqrt,
                     bias=inv_gamma[:, 0:1],
                     scale=1.0,
                 )
-            live["rsqrt", r] = rsqrt
-            for m in (0, 1):
-                nc.gpsimd.tensor_tensor(out=recip[:, m, :], in0=rsqrt[:, m, :], in1=rsqrt[:, m, :], op=ALU.mult)
 
-        def square_second_half(r):
-            nc.scalar.activation(out=live["recip", r][:, 2:4, :], in_=live["rsqrt", r][:, 2:4, :], func=ACT.Square)
+        def square_first_part(r):
+            engine = nc.vector if r == ROUNDS - 1 else nc.gpsimd
+            root = part(r, live["rsqrt", r], 0)
+            engine.tensor_tensor(out=part(r, live["recip", r], 0), in0=root, in1=root, op=ALU.mult)
 
-        def multiply_and_regroup(r):
-            live["squashed", r] = work.tile([P, ROWS, CHUNKS], BF16, name="squashed", align_bytes=64)
+        def square_second_part(r):
+            nc.scalar.activation(
+                out=part(r, live["recip", r], 1), in_=part(r, live["rsqrt", r], 1), func=ACT.Square
+            )
+
+        def multiply_and_regroup(r, first=0, last=ROWS):
+            if first == 0:
+                live["squashed", r] = work.tile([P, ROWS, CHUNKS], BF16, name="squashed", align_bytes=64)
+            runs = slice(first // RUN, last // RUN)
             nc.vector.tensor_tensor(
-                out=live["squashed", r][:].rearrange("p (c i) m -> p c m i", i=RUN),
-                in0=live["z", r][:].rearrange("p m (c i) -> p c m i", i=RUN),
-                in1=live["recip", r][:].rearrange("p m (c i) -> p c m i", i=RUN),
+                out=live["squashed", r][:].rearrange("p (c i) m -> p c m i", i=RUN)[:, runs],
+                in0=live["z", r][:].rearrange("p (m c i) -> p c m i", m=CHUNKS, i=RUN)[:, runs],
+                in1=live["recip", r][:].rearrange("p (m c i) -> p c m i", m=CHUNKS, i=RUN)[:, runs],
                 op=ALU.mult,
             )
 
-        def quantise_squashed(r):
-            live["s_codes", r] = work.tile([P, ROWS], U32, name="s_codes", align_bytes=64)
-            live["s_scales", r] = work.tile([P, ROWS], U8, name="s_scales", align_bytes=64)
+        def quantise_squashed(r, first=0, last=ROWS):
+            if first == 0:
+                live["s_codes", r] = work.tile([P, ROWS], U32, name="s_codes", align_bytes=64)
+                live["s_scales", r] = work.tile([P, ROWS], U8, name="s_scales", align_bytes=64)
             nc.vector.quantize_mx(
-                out=live["s_codes", r][:].bitcast(FP8X4),
-                scales=live["s_scales", r][:],
-                in_=live["squashed", r][:].rearrange("p s m -> p (s m)"),
+                out=live["s_codes", r][:, first:last].bitcast(FP8X4),
+                scales=live["s_scales", r][:, first:last],
+                in_=live["squashed", r][:, first:last, :].rearrange("p s m -> p (s m)"),
             )
 
         def scores(r):
@@ -194,19 +202,45 @@ def tile_decoder_pb_t_e_kernel(tc, hq1, hk1, proj1_words, proj1_scales, bias1, o
         with tc.manual_schedule():
             load_rows(0)
             load_constants()
-            for i in range(1 - LOAD_AHEAD, ROUNDS + 1):
+            load_words(0)
+            load_rows(1)
+            load_words(1)
+            for i in range(2 - LOAD_AHEAD, ROUNDS - 1):
                 when_valid(load_rows, i + LOAD_AHEAD)
                 when_valid(transpose_words, i + 2)
                 for m in range(CHUNKS):
                     when_valid(add_bias_and_residual, i, m)
-                when_valid(reciprocal_of_denominator, i)
+                if 0 <= i + 1 < H:
+                    regroup_weights(i + 1)
+                when_valid(reciprocal_roots, i)
+                when_valid(square_first_part, i)
                 when_valid(copy_words, i + 2, 1)
-                when_valid(square_second_half, i)
-                when_valid(multiply_and_regroup, i - 1)
+                when_valid(copy_and_store_scores, i - 3)
+                when_valid(square_second_part, i)
+                when_valid(multiply_and_regroup, i - 2)
                 when_valid(quantise_x, i + 1)
                 for m in range(CHUNKS):
                     when_valid(project, i + 1, m)
-                when_valid(quantise_squashed, i - 1)
-                when_valid(scores, i - 1)
+                when_valid(quantise_squashed, i - 2)
+                when_valid(scores, i - 2)
                 when_valid(copy_words, i + 2, 0)
-                when_valid(copy_and_store_scores, i - 1)
+
+            r = ROUNDS - 1
+            halves = ((0, S), (S, ROWS))
+            for first, last in halves:
+                for m in range(CHUNKS):
+                    add_bias_and_residual(r, m, first, last)
+            reciprocal_roots(r)
+            copy_and_store_scores(r - 3)
+            square_second_part(r)
+            for earlier in (r - 2, r - 1):
+                multiply_and_regroup(earlier)
+                quantise_squashed(earlier)
+                scores(earlier)
+                copy_and_store_scores(earlier)
+            square_first_part(r)
+            for first, last in halves:
+                multiply_and_regroup(r, first, last)
+                quantise_squashed(r, first, last)
+            scores(r)
+            copy_and_store_scores(r)

@@ -124,35 +124,45 @@ def tile_decoder_pb_t_e_kernel(tc, hq1, hk1, proj1_words, proj1_scales, bias1, o
                 op1=ALU.add,
             )
 
-        def part(r, tile, k):
+        def pieces(r, tile):
+            if r == 0:
+                return [tile[:, 0 : 2 * ROWS], tile[:, 2 * ROWS :]]
             if r == ROUNDS - 1:
-                return tile[:].rearrange("p (m s) -> p m s", m=CHUNKS)[:, :, S * k : S * (k + 1)]
-            return tile[:, GPSIMD_SHARE:] if k else tile[:, 0:GPSIMD_SHARE]
+                rows = tile[:].rearrange("p (m s) -> p m s", m=CHUNKS)
+                return [rows[:, :, 0:S], rows[:, :, S:ROWS]]
+            return [tile[:]]
+
+        def magnitudes(r):
+            live["magnitude", r] = work.tile([P, CHUNKS * ROWS], F32, name="magnitude")
+            for z, magnitude in zip(pieces(r, live["z", r]), pieces(r, live["magnitude", r])):
+                nc.scalar.activation(out=magnitude, in_=z, func=ACT.Abs)
 
         def reciprocal_roots(r):
-            magnitude = work.tile([P, CHUNKS * ROWS], F32, name="magnitude")
-            live["rsqrt", r] = work.tile([P, CHUNKS * ROWS], F32, name="rsqrt")
-            live["recip", r] = work.tile([P, CHUNKS * ROWS], F32, name="recip", bufs=3)
-            for k in range(2):
-                nc.scalar.activation(out=part(r, magnitude, k), in_=part(r, live["z", r], k), func=ACT.Abs)
-            for k in range(2):
+            live["root", r] = work.tile([P, CHUNKS * ROWS], F32, name="root")
+            for magnitude, root in zip(pieces(r, live["magnitude", r]), pieces(r, live["root", r])):
                 nc.scalar.activation(
-                    out=part(r, live["rsqrt", r], k),
-                    in_=part(r, magnitude, k),
-                    func=ACT.Abs_reciprocal_sqrt,
-                    bias=inv_gamma[:, 0:1],
-                    scale=1.0,
+                    out=root, in_=magnitude, func=ACT.Abs_reciprocal_sqrt, bias=inv_gamma[:, 0:1], scale=1.0
                 )
 
-        def square_first_part(r):
-            engine = nc.vector if r == ROUNDS - 1 else nc.gpsimd
-            root = part(r, live["rsqrt", r], 0)
-            engine.tensor_tensor(out=part(r, live["recip", r], 0), in0=root, in1=root, op=ALU.mult)
+        def square_on_gpsimd(r):
+            live["recip", r] = work.tile([P, CHUNKS * ROWS], F32, name="recip", bufs=3)
+            root = live["root", r][:, 0:GPSIMD_SHARE]
+            nc.gpsimd.tensor_tensor(out=live["recip", r][:, 0:GPSIMD_SHARE], in0=root, in1=root, op=ALU.mult)
 
-        def square_second_part(r):
+        def square_on_scalar(r):
             nc.scalar.activation(
-                out=part(r, live["recip", r], 1), in_=part(r, live["rsqrt", r], 1), func=ACT.Square
+                out=live["recip", r][:, GPSIMD_SHARE:], in_=live["root", r][:, GPSIMD_SHARE:], func=ACT.Square
             )
+
+        def square_last_round(k):
+            r = ROUNDS - 1
+            if k == 0:
+                live["recip", r] = work.tile([P, CHUNKS * ROWS], F32, name="recip", bufs=3)
+            root, recip = pieces(r, live["root", r])[k], pieces(r, live["recip", r])[k]
+            if k == 0:
+                nc.vector.tensor_tensor(out=recip, in0=root, in1=root, op=ALU.mult)
+            else:
+                nc.scalar.activation(out=recip, in_=root, func=ACT.Square)
 
         def multiply_and_regroup(r, first=0, last=ROWS):
             if first == 0:
@@ -212,17 +222,18 @@ def tile_decoder_pb_t_e_kernel(tc, hq1, hk1, proj1_words, proj1_scales, bias1, o
                     when_valid(add_bias_and_residual, i, m)
                 if 0 <= i + 1 < H:
                     regroup_weights(i + 1)
-                when_valid(reciprocal_roots, i)
-                when_valid(square_first_part, i)
-                when_valid(copy_words, i + 2, 1)
-                when_valid(copy_and_store_scores, i - 3)
-                when_valid(square_second_part, i)
-                when_valid(multiply_and_regroup, i - 2)
                 when_valid(quantise_x, i + 1)
                 for m in range(CHUNKS):
                     when_valid(project, i + 1, m)
-                when_valid(quantise_squashed, i - 2)
-                when_valid(scores, i - 2)
+                when_valid(quantise_squashed, i - 3)
+                when_valid(scores, i - 3)
+                when_valid(copy_words, i + 2, 1)
+                when_valid(copy_and_store_scores, i - 3)
+                when_valid(magnitudes, i)
+                when_valid(square_on_scalar, i - 1)
+                when_valid(reciprocal_roots, i)
+                when_valid(square_on_gpsimd, i)
+                when_valid(multiply_and_regroup, i - 2)
                 when_valid(copy_words, i + 2, 0)
 
             r = ROUNDS - 1
@@ -230,17 +241,24 @@ def tile_decoder_pb_t_e_kernel(tc, hq1, hk1, proj1_words, proj1_scales, bias1, o
             for first, last in halves:
                 for m in range(CHUNKS):
                     add_bias_and_residual(r, m, first, last)
-            reciprocal_roots(r)
+            quantise_squashed(r - 3)
+            scores(r - 3)
             copy_and_store_scores(r - 3)
-            square_second_part(r)
+            square_on_scalar(r - 1)
+            magnitudes(r)
+            reciprocal_roots(r)
+            multiply_and_regroup(r - 2)
+            quantise_squashed(r - 2)
+            multiply_and_regroup(r - 1)
+            square_last_round(0)
+            square_last_round(1)
+            quantise_squashed(r - 1)
             for earlier in (r - 2, r - 1):
-                multiply_and_regroup(earlier)
-                quantise_squashed(earlier)
                 scores(earlier)
                 copy_and_store_scores(earlier)
-            square_first_part(r)
             for first, last in halves:
                 multiply_and_regroup(r, first, last)
+            for first, last in halves:
                 quantise_squashed(r, first, last)
             scores(r)
             copy_and_store_scores(r)

@@ -20,7 +20,7 @@ ROWS = 2 * S
 ROW_TILES = ROWS // P
 CHUNKS = D // P
 GAMMA = 64.0
-GPSIMD_SHARE = 1152
+GPSIMD_SHARE = 1280
 RUN = 4
 LOAD_AHEAD = 4
 
@@ -62,9 +62,9 @@ def tile_decoder_pb_t_e_kernel(tc, hq1, hk1, proj1_words, proj1_scales, bias1, o
         def load_words(h):
             nc.sync.dma_start(out=words_raw[:, h, :], in_=proj1_words[h].rearrange("p n t -> p (n t)").bitcast(I32))
 
-        def regroup_weights(h):
-            nc.vector.tensor_copy(out=w_words[:, h], in_=words_raw[:, h, :].rearrange("p (j m) -> p m j", m=CHUNKS))
-            nc.vector.tensor_copy(out=w_scales[:, h], in_=scales_raw[:, h, :].rearrange("p (j m) -> p m j", m=CHUNKS))
+        def regroup_weights(h, engine):
+            engine.tensor_copy(out=w_words[:, h], in_=words_raw[:, h, :].rearrange("p (j m) -> p m j", m=CHUNKS))
+            engine.tensor_copy(out=w_scales[:, h], in_=scales_raw[:, h, :].rearrange("p (j m) -> p m j", m=CHUNKS))
 
         def load_rows(r):
             b, h = divmod(r, H)
@@ -144,10 +144,10 @@ def tile_decoder_pb_t_e_kernel(tc, hq1, hk1, proj1_words, proj1_scales, bias1, o
                     out=root, in_=magnitude, func=ACT.Abs_reciprocal_sqrt, bias=inv_gamma[:, 0:1], scale=1.0
                 )
 
-        def square_on_gpsimd(r):
+        def square_on_gpsimd(r, engine=nc.gpsimd):
             live["recip", r] = work.tile([P, CHUNKS * ROWS], F32, name="recip", bufs=3)
             root = live["root", r][:, 0:GPSIMD_SHARE]
-            nc.gpsimd.tensor_tensor(out=live["recip", r][:, 0:GPSIMD_SHARE], in0=root, in1=root, op=ALU.mult)
+            engine.tensor_tensor(out=live["recip", r][:, 0:GPSIMD_SHARE], in0=root, in1=root, op=ALU.mult)
 
         def square_on_scalar(r):
             nc.scalar.activation(
@@ -215,24 +215,29 @@ def tile_decoder_pb_t_e_kernel(tc, hq1, hk1, proj1_words, proj1_scales, bias1, o
             load_words(0)
             load_rows(1)
             load_words(1)
+            regroup_weights(1, nc.gpsimd)
             for i in range(2 - LOAD_AHEAD, ROUNDS - 1):
                 when_valid(load_rows, i + LOAD_AHEAD)
                 when_valid(transpose_words, i + 2)
                 for m in range(CHUNKS):
                     when_valid(add_bias_and_residual, i, m)
-                if 0 <= i + 1 < H:
-                    regroup_weights(i + 1)
+                if i == -1:
+                    regroup_weights(0, nc.vector)
                 when_valid(quantise_x, i + 1)
                 for m in range(CHUNKS):
                     when_valid(project, i + 1, m)
                 when_valid(quantise_squashed, i - 3)
                 when_valid(scores, i - 3)
-                when_valid(copy_words, i + 2, 1)
+                if i != 0:
+                    when_valid(copy_words, i + 2, 1)
                 when_valid(copy_and_store_scores, i - 3)
                 when_valid(magnitudes, i)
+                if i == 0:
+                    copy_words(2, 1)
                 when_valid(square_on_scalar, i - 1)
                 when_valid(reciprocal_roots, i)
-                when_valid(square_on_gpsimd, i)
+                if i < ROUNDS - 2:
+                    when_valid(square_on_gpsimd, i)
                 when_valid(multiply_and_regroup, i - 2)
                 when_valid(copy_words, i + 2, 0)
 
@@ -244,10 +249,11 @@ def tile_decoder_pb_t_e_kernel(tc, hq1, hk1, proj1_words, proj1_scales, bias1, o
             quantise_squashed(r - 3)
             scores(r - 3)
             copy_and_store_scores(r - 3)
+            multiply_and_regroup(r - 2)
+            square_on_gpsimd(r - 1, nc.vector)
             square_on_scalar(r - 1)
             magnitudes(r)
             reciprocal_roots(r)
-            multiply_and_regroup(r - 2)
             quantise_squashed(r - 2)
             multiply_and_regroup(r - 1)
             square_last_round(0)

@@ -20,8 +20,9 @@ ROWS = 2 * S
 ROW_TILES = ROWS // P
 CHUNKS = D // P
 GAMMA = 64.0
-GPSIMD_SHARE = 1280
+GPSIMD_SHARE = 1216
 RUN = 4
+SQUASH_LAG = 4
 LOAD_AHEAD = 4
 
 FLOPS = 2 * (2 * B * H * S * D * D) + 2 * B * H * S * S * D
@@ -83,19 +84,24 @@ def tile_decoder_pb_t_e_kernel(tc, hq1, hk1, proj1_words, proj1_scales, bias1, o
 
         def copy_words(r, half):
             if half == 1:
-                live["x_grouped", r] = work.tile([P, ROWS * PACK], BF16, name="x_grouped", align_bytes=64, bufs=3)
-            grouped_words = live["x_grouped", r][:].bitcast(F32).rearrange("p (s u) -> p s u", u=2)
+                live["to_quantise", r] = work.tile([P, 2, ROWS * PACK], BF16, name="to_quantise", align_bytes=64, bufs=3)
+            grouped_words = live["to_quantise", r][:, 0, :].bitcast(F32).rearrange("p (s u) -> p s u", u=2)
             copy = nc.scalar.copy if half else nc.vector.tensor_copy
             copy(
                 out=grouped_words[:, S * half : S * (half + 1), :],
                 in_=live["words_ps", r, half][:].rearrange("p u s -> p s u"),
             )
 
-        def quantise_x(r):
-            live["x_codes", r] = work.tile([P, ROWS], U32, name="x_codes", align_bytes=64)
-            live["x_scales", r] = work.tile([P, ROWS], U8, name="x_scales", align_bytes=64)
+        def quantise(r):
+            parts = 2 if r >= SQUASH_LAG else 1
+            codes = work.tile([P, 2, ROWS], U32, name="codes", align_bytes=64)
+            scales = work.tile([P, 2, ROWS], U8, name="scales", align_bytes=64)
+            live["x_codes", r], live["x_scales", r] = codes[:, 0, :], scales[:, 0, :]
+            live["s_codes", r - SQUASH_LAG], live["s_scales", r - SQUASH_LAG] = codes[:, 1, :], scales[:, 1, :]
             nc.vector.quantize_mx(
-                out=live["x_codes", r][:].bitcast(FP8X4), scales=live["x_scales", r][:], in_=live["x_grouped", r][:]
+                out=codes[:, 0:parts, :].rearrange("p a s -> p (a s)").bitcast(FP8X4),
+                scales=scales[:, 0:parts, :].rearrange("p a s -> p (a s)"),
+                in_=live["to_quantise", r][:, 0:parts, :].rearrange("p a k -> p (a k)"),
             )
 
         def project(r, m):
@@ -105,8 +111,8 @@ def tile_decoder_pb_t_e_kernel(tc, hq1, hk1, proj1_words, proj1_scales, bias1, o
                 out=live["proj_ps", r, m][:],
                 lhsT=w_words[:, h, m, :].bitcast(FP8X4),
                 lhsT_scale=w_scales[:, h, m, :],
-                rhs=live["x_codes", r][:].bitcast(FP8X4),
-                rhs_scale=live["x_scales", r][:],
+                rhs=live["x_codes", r].bitcast(FP8X4),
+                rhs_scale=live["x_scales", r],
                 start=True,
                 stop=True,
             )
@@ -119,7 +125,7 @@ def tile_decoder_pb_t_e_kernel(tc, hq1, hk1, proj1_words, proj1_scales, bias1, o
                 out=live["z", r][:, ROWS * m + first : ROWS * m + last],
                 in0=live["proj_ps", r, m][:, first:last],
                 scalar=bias_col[:, h, m : m + 1],
-                in1=live["x_grouped", r][:].rearrange("p (s m) -> p m s", m=PACK)[:, m, first:last],
+                in1=live["to_quantise", r][:, 0, :].rearrange("p (s m) -> p m s", m=PACK)[:, m, first:last],
                 op0=ALU.add,
                 op1=ALU.add,
             )
@@ -165,11 +171,13 @@ def tile_decoder_pb_t_e_kernel(tc, hq1, hk1, proj1_words, proj1_scales, bias1, o
                 nc.scalar.activation(out=recip, in_=root, func=ACT.Square)
 
         def multiply_and_regroup(r, first=0, last=ROWS):
-            if first == 0:
-                live["squashed", r] = work.tile([P, ROWS, CHUNKS], BF16, name="squashed", align_bytes=64)
+            if r + SQUASH_LAG < ROUNDS:
+                live["squashed", r] = live["to_quantise", r + SQUASH_LAG][:, 1, :]
+            elif first == 0:
+                live["squashed", r] = work.tile([P, ROWS * CHUNKS], BF16, name="squashed", align_bytes=64)[:]
             runs = slice(first // RUN, last // RUN)
             nc.vector.tensor_tensor(
-                out=live["squashed", r][:].rearrange("p (c i) m -> p c m i", i=RUN)[:, runs],
+                out=live["squashed", r].rearrange("p (c i m) -> p c m i", i=RUN, m=CHUNKS)[:, runs],
                 in0=live["z", r][:].rearrange("p (m c i) -> p c m i", m=CHUNKS, i=RUN)[:, runs],
                 in1=live["recip", r][:].rearrange("p (m c i) -> p c m i", m=CHUNKS, i=RUN)[:, runs],
                 op=ALU.mult,
@@ -177,12 +185,12 @@ def tile_decoder_pb_t_e_kernel(tc, hq1, hk1, proj1_words, proj1_scales, bias1, o
 
         def quantise_squashed(r, first=0, last=ROWS):
             if first == 0:
-                live["s_codes", r] = work.tile([P, ROWS], U32, name="s_codes", align_bytes=64)
-                live["s_scales", r] = work.tile([P, ROWS], U8, name="s_scales", align_bytes=64)
+                live["s_codes", r] = work.tile([P, ROWS], U32, name="s_codes", align_bytes=64)[:]
+                live["s_scales", r] = work.tile([P, ROWS], U8, name="s_scales", align_bytes=64)[:]
             nc.vector.quantize_mx(
                 out=live["s_codes", r][:, first:last].bitcast(FP8X4),
                 scales=live["s_scales", r][:, first:last],
-                in_=live["squashed", r][:, first:last, :].rearrange("p s m -> p (s m)"),
+                in_=live["squashed", r][:, PACK * first : PACK * last],
             )
 
         def scores(r):
@@ -201,7 +209,7 @@ def tile_decoder_pb_t_e_kernel(tc, hq1, hk1, proj1_words, proj1_scales, bias1, o
 
         def copy_and_store_scores(r):
             b, h = divmod(r, H)
-            result = work.tile([P, S // P, S], F32, name="result")
+            result = work.tile([P, S // P, S], F32, name="result", bufs=4)
             nc.scalar.copy(out=result[:], in_=live["score_ps", r][:])
             nc.sync.dma_start(out=out[b, h].rearrange("(t p) k -> p t k", p=P), in_=result[:])
 
@@ -223,15 +231,14 @@ def tile_decoder_pb_t_e_kernel(tc, hq1, hk1, proj1_words, proj1_scales, bias1, o
                     when_valid(add_bias_and_residual, i, m)
                 if i == -1:
                     regroup_weights(0, nc.vector)
-                when_valid(quantise_x, i + 1)
+                when_valid(quantise, i + 1)
                 for m in range(CHUNKS):
                     when_valid(project, i + 1, m)
-                when_valid(quantise_squashed, i - 3)
                 when_valid(scores, i - 3)
                 if i != 0:
                     when_valid(copy_words, i + 2, 1)
-                when_valid(copy_and_store_scores, i - 3)
                 when_valid(magnitudes, i)
+                when_valid(copy_and_store_scores, i - 3)
                 if i == 0:
                     copy_words(2, 1)
                 when_valid(square_on_scalar, i - 1)

from contextlib import ExitStack

import concourse.masks as masks
import concourse.mybir as mybir

F32 = mybir.dt.float32
BF16 = mybir.dt.bfloat16
I32 = mybir.dt.int32
U8 = mybir.dt.uint8
U32 = mybir.dt.uint32
FP8X4 = mybir.dt.float8_e4m3fn_x4
ACT = mybir.ActivationFunctionType
ALU = mybir.AluOpType

P = 128
PACK = 4
B, H, S, D = 16, 2, 256, 512
ROUNDS = B * H
ROWS = 2 * S
ROW_TILES = ROWS // P
CHUNKS = D // P
GAMMA = 64.0
GPSIMD_SHARE = 1216
RUN = 4
SQUASH_LAG = 4
LOAD_AHEAD = 4

FLOPS = 2 * (2 * B * H * S * D * D) + 2 * B * H * S * S * D


def tile_decoder_pb_t_e_kernel(tc, hq1, hk1, proj1_words, proj1_scales, bias1, out):
    nc = tc.nc
    with ExitStack() as ctx:
        const = ctx.enter_context(tc.tile_pool(name="const", bufs=1))
        loads = ctx.enter_context(tc.tile_pool(name="loads", bufs=LOAD_AHEAD))
        work = ctx.enter_context(tc.tile_pool(name="work", bufs=2))
        words_psum = ctx.enter_context(tc.psum_pool(name="words_psum", bufs=3))
        proj_psum = ctx.enter_context(tc.psum_pool(name="proj_psum", bufs=4))
        score_psum = ctx.enter_context(tc.psum_pool(name="score_psum", bufs=1))

        ident_f32 = const.tile([P, P], F32, name="ident_f32")
        inv_gamma = const.tile([P, 1], F32, name="inv_gamma")
        words_raw = const.tile([P, H, D], I32, name="words_raw", align_bytes=64)
        scales_raw = const.tile([P, H, D], U8, name="scales_raw", align_bytes=64)
        w_words = const.tile([P, H, CHUNKS, P], I32, name="w_words", align_bytes=64)
        w_scales = const.tile([P, H, CHUNKS, P], U8, name="w_scales", align_bytes=64)
        bias_col = const.tile([P, H, CHUNKS], BF16, name="bias_col")

        live = {}

        def load_constants():
            masks.make_identity(nc, ident_f32[:])
            nc.vector.memset(inv_gamma[:], 1.0 / GAMMA)

            nc.vector.memset(scales_raw[:].rearrange("p h n -> p (h n)").bitcast(I32), 0)
            for quadrant in range(4):
                nc.sync.dma_start(
                    out=scales_raw[32 * quadrant : 32 * quadrant + 4, :, :].bitcast(I32),
                    in_=proj1_scales[:, 4 * quadrant : 4 * quadrant + 4, :].rearrange("h r n -> r h n").bitcast(I32),
                )
            nc.sync.dma_start(out=bias_col[:], in_=bias1.rearrange("a h c (j m) -> j (a h c) m", m=CHUNKS))

        def load_words(h):
            nc.sync.dma_start(out=words_raw[:, h, :], in_=proj1_words[h].rearrange("p n t -> p (n t)").bitcast(I32))

        def regroup_weights(h, engine):
            engine.tensor_copy(out=w_words[:, h], in_=words_raw[:, h, :].rearrange("p (j m) -> p m j", m=CHUNKS))
            engine.tensor_copy(out=w_scales[:, h], in_=scales_raw[:, h, :].rearrange("p (j m) -> p m j", m=CHUNKS))

        def load_rows(r):
            b, h = divmod(r, H)
            live["x", r] = loads.tile([P, ROW_TILES, D], BF16, name="x")
            nc.sync.dma_start(out=live["x", r][:, 0:2, :], in_=hq1[b, h].rearrange("(t p) d -> p t d", p=P))
            nc.sync.dma_start(out=live["x", r][:, 2:4, :], in_=hk1[b, h].rearrange("(t p) d -> p t d", p=P))

        def transpose_words(r):
            for half in range(2):
                words_ps = words_psum.tile([P, 2, S], F32, name="words_ps")
                live["words_ps", r, half] = words_ps
                for i in range(2):
                    words = live["x", r][:, 2 * half + i, :].bitcast(F32)
                    for u in range(2):
                        nc.tensor.transpose(words_ps[:, u, P * i : P * (i + 1)], words[:, u : D // 2 : 2], ident_f32[:])

        def copy_words(r, half):
            if half == 1:
                live["to_quantise", r] = work.tile([P, 2, ROWS * PACK], BF16, name="to_quantise", align_bytes=64, bufs=3)
            grouped_words = live["to_quantise", r][:, 0, :].bitcast(F32).rearrange("p (s u) -> p s u", u=2)
            copy = nc.scalar.copy if half else nc.vector.tensor_copy
            copy(
                out=grouped_words[:, S * half : S * (half + 1), :],
                in_=live["words_ps", r, half][:].rearrange("p u s -> p s u"),
            )

        def quantise(r):
            parts = 2 if r >= SQUASH_LAG else 1
            codes = work.tile([P, 2, ROWS], U32, name="codes", align_bytes=64)
            scales = work.tile([P, 2, ROWS], U8, name="scales", align_bytes=64)
            live["x_codes", r], live["x_scales", r] = codes[:, 0, :], scales[:, 0, :]
            live["s_codes", r - SQUASH_LAG], live["s_scales", r - SQUASH_LAG] = codes[:, 1, :], scales[:, 1, :]
            nc.vector.quantize_mx(
                out=codes[:, 0:parts, :].rearrange("p a s -> p (a s)").bitcast(FP8X4),
                scales=scales[:, 0:parts, :].rearrange("p a s -> p (a s)"),
                in_=live["to_quantise", r][:, 0:parts, :].rearrange("p a k -> p (a k)"),
            )

        def project(r, m):
            h = r % H
            live["proj_ps", r, m] = proj_psum.tile([P, ROWS], F32, name="proj_ps")
            nc.tensor.matmul_mx(
                out=live["proj_ps", r, m][:],
                lhsT=w_words[:, h, m, :].bitcast(FP8X4),
                lhsT_scale=w_scales[:, h, m, :],
                rhs=live["x_codes", r].bitcast(FP8X4),
                rhs_scale=live["x_scales", r],
                start=True,
                stop=True,
            )

        def add_bias_and_residual(r, m, first=0, last=ROWS):
            h = r % H
            if m == 0 and first == 0:
                live["z", r] = work.tile([P, CHUNKS * ROWS], F32, name="z", bufs=3)
            nc.vector.scalar_tensor_tensor(
                out=live["z", r][:, ROWS * m + first : ROWS * m + last],
                in0=live["proj_ps", r, m][:, first:last],
                scalar=bias_col[:, h, m : m + 1],
                in1=live["to_quantise", r][:, 0, :].rearrange("p (s m) -> p m s", m=PACK)[:, m, first:last],
                op0=ALU.add,
                op1=ALU.add,
            )

        def pieces(r, tile):
            if r == 0:
                return [tile[:, 0 : 2 * ROWS], tile[:, 2 * ROWS :]]
            if r == ROUNDS - 1:
                rows = tile[:].rearrange("p (m s) -> p m s", m=CHUNKS)
                return [rows[:, :, 0:S], rows[:, :, S:ROWS]]
            return [tile[:]]

        def magnitudes(r):
            live["magnitude", r] = work.tile([P, CHUNKS * ROWS], F32, name="magnitude")
            for z, magnitude in zip(pieces(r, live["z", r]), pieces(r, live["magnitude", r])):
                nc.scalar.activation(out=magnitude, in_=z, func=ACT.Abs)

        def reciprocal_roots(r):
            live["root", r] = work.tile([P, CHUNKS * ROWS], F32, name="root")
            for magnitude, root in zip(pieces(r, live["magnitude", r]), pieces(r, live["root", r])):
                nc.scalar.activation(
                    out=root, in_=magnitude, func=ACT.Abs_reciprocal_sqrt, bias=inv_gamma[:, 0:1], scale=1.0
                )

        def square_on_gpsimd(r, engine=nc.gpsimd):
            live["recip", r] = work.tile([P, CHUNKS * ROWS], F32, name="recip", bufs=3)
            root = live["root", r][:, 0:GPSIMD_SHARE]
            engine.tensor_tensor(out=live["recip", r][:, 0:GPSIMD_SHARE], in0=root, in1=root, op=ALU.mult)

        def square_on_scalar(r):
            nc.scalar.activation(
                out=live["recip", r][:, GPSIMD_SHARE:], in_=live["root", r][:, GPSIMD_SHARE:], func=ACT.Square
            )

        def square_last_round(k):
            r = ROUNDS - 1
            if k == 0:
                live["recip", r] = work.tile([P, CHUNKS * ROWS], F32, name="recip", bufs=3)
            root, recip = pieces(r, live["root", r])[k], pieces(r, live["recip", r])[k]
            if k == 0:
                nc.vector.tensor_tensor(out=recip, in0=root, in1=root, op=ALU.mult)
            else:
                nc.scalar.activation(out=recip, in_=root, func=ACT.Square)

        def multiply_and_regroup(r, first=0, last=ROWS):
            if r + SQUASH_LAG < ROUNDS:
                live["squashed", r] = live["to_quantise", r + SQUASH_LAG][:, 1, :]
            elif first == 0:
                live["squashed", r] = work.tile([P, ROWS * CHUNKS], BF16, name="squashed", align_bytes=64)[:]
            runs = slice(first // RUN, last // RUN)
            nc.vector.tensor_tensor(
                out=live["squashed", r].rearrange("p (c i m) -> p c m i", i=RUN, m=CHUNKS)[:, runs],
                in0=live["z", r][:].rearrange("p (m c i) -> p c m i", m=CHUNKS, i=RUN)[:, runs],
                in1=live["recip", r][:].rearrange("p (m c i) -> p c m i", m=CHUNKS, i=RUN)[:, runs],
                op=ALU.mult,
            )

        def quantise_squashed(r, first=0, last=ROWS):
            if first == 0:
                live["s_codes", r] = work.tile([P, ROWS], U32, name="s_codes", align_bytes=64)[:]
                live["s_scales", r] = work.tile([P, ROWS], U8, name="s_scales", align_bytes=64)[:]
            nc.vector.quantize_mx(
                out=live["s_codes", r][:, first:last].bitcast(FP8X4),
                scales=live["s_scales", r][:, first:last],
                in_=live["squashed", r][:, PACK * first : PACK * last],
            )

        def scores(r):
            codes, scales = live["s_codes", r], live["s_scales", r]
            live["score_ps", r] = score_psum.tile([P, S // P, S], F32, name="score_ps")
            for t in range(S // P):
                nc.tensor.matmul_mx(
                    out=live["score_ps", r][:, t, :],
                    lhsT=codes[:, P * t : P * (t + 1)].bitcast(FP8X4),
                    lhsT_scale=scales[:, P * t : P * (t + 1)],
                    rhs=codes[:, S : 2 * S].bitcast(FP8X4),
                    rhs_scale=scales[:, S : 2 * S],
                    start=True,
                    stop=True,
                )

        def copy_and_store_scores(r):
            b, h = divmod(r, H)
            result = work.tile([P, S // P, S], F32, name="result", bufs=4)
            nc.scalar.copy(out=result[:], in_=live["score_ps", r][:])
            nc.sync.dma_start(out=out[b, h].rearrange("(t p) k -> p t k", p=P), in_=result[:])

        def when_valid(stage, r, *part):
            if 0 <= r < ROUNDS:
                stage(r, *part)

        with tc.manual_schedule():
            load_rows(0)
            load_constants()
            load_words(0)
            load_rows(1)
            load_words(1)
            regroup_weights(1, nc.gpsimd)
            for i in range(2 - LOAD_AHEAD, ROUNDS - 1):
                when_valid(load_rows, i + LOAD_AHEAD)
                when_valid(transpose_words, i + 2)
                for m in range(CHUNKS):
                    when_valid(add_bias_and_residual, i, m)
                if i == -1:
                    regroup_weights(0, nc.vector)
                when_valid(quantise, i + 1)
                for m in range(CHUNKS):
                    when_valid(project, i + 1, m)
                when_valid(scores, i - 3)
                if i != 0:
                    when_valid(copy_words, i + 2, 1)
                when_valid(magnitudes, i)
                when_valid(copy_and_store_scores, i - 3)
                if i == 0:
                    copy_words(2, 1)
                when_valid(square_on_scalar, i - 1)
                when_valid(reciprocal_roots, i)
                if i < ROUNDS - 2:
                    when_valid(square_on_gpsimd, i)
                when_valid(multiply_and_regroup, i - 2)
                when_valid(copy_words, i + 2, 0)

            r = ROUNDS - 1
            halves = ((0, S), (S, ROWS))
            for first, last in halves:
                for m in range(CHUNKS):
                    add_bias_and_residual(r, m, first, last)
            quantise_squashed(r - 3)
            scores(r - 3)
            copy_and_store_scores(r - 3)
            multiply_and_regroup(r - 2)
            square_on_gpsimd(r - 1, nc.vector)
            square_on_scalar(r - 1)
            magnitudes(r)
            reciprocal_roots(r)
            quantise_squashed(r - 2)
            multiply_and_regroup(r - 1)
            square_last_round(0)
            square_last_round(1)
            quantise_squashed(r - 1)
            for earlier in (r - 2, r - 1):
                scores(earlier)
                copy_and_store_scores(earlier)
            for first, last in halves:
                multiply_and_regroup(r, first, last)
            for first, last in halves:
                quantise_squashed(r, first, last)
            scores(r)
            copy_and_store_scores(r)
